import numpy as np
import ml_dtypes


def mxq(x, axis, fmt="e4m3"):
    dtype, down = {"e4m3": (ml_dtypes.float8_e4m3fn, 7), "e5m2": (ml_dtypes.float8_e5m2, 14)}[fmt]
    v = np.moveaxis(np.asarray(x, np.float32).astype(ml_dtypes.bfloat16).astype(np.float64), axis, -1)
    blocks = v.reshape(v.shape[:-1] + (-1, 32))
    amax = np.abs(blocks).max(-1, keepdims=True)
    byte = np.maximum(np.where(amax > 0, np.frexp(amax)[1] - 1 + 127, 0) - down, 1)
    scale = np.exp2(byte - 127.0)
    codes = (blocks / scale).astype(np.float32).astype(dtype).astype(np.float64)
    return np.moveaxis((codes * scale).reshape(v.shape), -1, axis)


WIDE = False


def mx_kscale(k):
    if not WIDE:
        return np.ones(k)
    levels = np.array([10, -10, 5, -5, 0])
    a = np.random.permutation(np.resize(levels, k // 512 * 4)).reshape(k // 512, 4)
    idx = np.arange(k)
    return np.exp2(a[idx // 512, idx % 128 // 32])


BF16 = ml_dtypes.bfloat16


def bf(x):
    return np.asarray(x, np.float32).astype(BF16)


def f64(x):
    return np.asarray(x).astype(np.float64)


B, IN, HID, PROJ, H, KC = 4096, 2048, 128, 512, 1, 4
BH = HID // H
BI = PROJ // H


def sigmoid(v):
    return 1.0 / (1.0 + np.exp(-v))


def silu(v):
    return v / (1.0 + np.exp(-v))


def blockdiag(vq, w, b):
    y = vq.reshape(B, H, BI).transpose(1, 0, 2) @ mxq(f64(w), 1, "e4m3")
    return y.transpose(1, 0, 2).reshape(B, HID) + f64(b)


def setup_inputs():
    s, t = mx_kscale(PROJ), mx_kscale(PROJ)
    sh, th = s.reshape(H, BI, 1), t.reshape(H, BI, 1)
    r = np.random.standard_normal
    return {"x_conv": bf(silu(r((B, PROJ))) * s), "x_left": bf(r((B, PROJ)) * t),
            "c_prev": bf(r((B, HID))), "n_prev": bf(r((B, HID))), "m_prev": bf(0.5 * r((B, HID))),
            "wq_w": bf(r((H, BI, BH)) * 1.5 / np.sqrt(BI) / sh), "wq_b": bf(0.2 * r(HID)),
            "wk_w": bf(r((H, BI, BH)) * 0.5 * np.sqrt(BH) / np.sqrt(BI) / sh), "wk_b": bf(0.1 * np.sqrt(BH) * r(HID)),
            "wv_w": bf(r((H, BI, BH)) / np.sqrt(BI) / th), "wv_b": bf(0.2 * r(HID)),
            "wi_w": bf(r((PROJ, HID)) * 1.5 / np.sqrt(PROJ) / s[:, None]), "wi_b": bf(0.2 * r(HID)),
            "wf_w": bf(r((PROJ, HID)) * 1.5 / np.sqrt(PROJ) / s[:, None]), "wf_b": bf(0.2 * r(HID)),
            "wo_w": bf(r((PROJ, HID)) / np.sqrt(PROJ) / t[:, None]), "wo_b": bf(0.2 * r(HID))}


def reference(x_conv, x_left, c_prev, n_prev, m_prev, wq_w, wq_b, wk_w, wk_b, wv_w, wv_b, wi_w, wi_b, wf_w, wf_b, wo_w, wo_b):
    xc = mxq(f64(x_conv), 1, "e4m3")
    xl = mxq(f64(x_left), 1, "e4m3")
    q = blockdiag(xc, wq_w, wq_b)
    k = blockdiag(xc, wk_w, wk_b) / np.sqrt(BH)
    v = blockdiag(xl, wv_w, wv_b)
    i_tilde = (xc @ mxq(f64(wi_w), 0, "e4m3")) + f64(wi_b)
    f_tilde = (xc @ mxq(f64(wf_w), 0, "e4m3")) + f64(wf_b)
    o = sigmoid((xl @ mxq(f64(wo_w), 0, "e4m3")) + f64(wo_b))
    m_t = np.maximum(f_tilde + f64(m_prev), i_tilde)
    i = np.exp(i_tilde - m_t)
    f = np.exp(f_tilde + f64(m_prev) - m_t)
    c_t = f * f64(c_prev) + i * (v * k)
    n_t = f * f64(n_prev) + i * k
    denom = np.sqrt(np.sum((n_t * q) ** 2, axis=-1, keepdims=True)) + 1e-6
    h_t = o * (c_t * q) / denom
    return h_t, c_t, n_t, m_t

@@ -1,0 +1,311 @@
+import math
+
+import concourse.mybir as mybir
+from concourse.masks import make_identity
+
+FP8X4 = mybir.dt.float8_e4m3fn_x4
+BF16 = mybir.dt.bfloat16
+F32 = mybir.dt.float32
+U32 = mybir.dt.uint32
+U8 = mybir.dt.uint8
+ALU = mybir.AluOpType
+ACT = mybir.ActivationFunctionType
+
+P = 128
+B = 4096
+K = 512
+H = 128
+NT = B // P
+TPC = 4
+NCH = NT // TPC
+CW = TPC * H
+FLOPS = 2 * B * K * H * 6
+
+
+def tile_mlstmblock_pb_t_kernel(
+    tc,
+    x_conv,
+    x_left,
+    c_prev,
+    n_prev,
+    m_prev,
+    wq_w,
+    wq_b,
+    wk_w,
+    wk_b,
+    wv_w,
+    wv_b,
+    wi_w,
+    wi_b,
+    wf_w,
+    wf_b,
+    wo_w,
+    wo_b,
+    out_0,
+    out_1,
+    out_2,
+    out_3,
+):
+    nc = tc.nc
+    k_scale = 1.0 / math.sqrt(float(H))
+
+    xc_v = x_conv.rearrange("(p t) k -> p t k", t=NT)
+    xl_v = x_left.rearrange("(p t) k -> p t k", t=NT)
+    c_v = c_prev.rearrange("(p t) h -> p t h", t=NT)
+    n_v = n_prev.rearrange("(p t) h -> p t h", t=NT)
+    m_v = m_prev.rearrange("(p t) h -> p t h", t=NT)
+    h_ov = out_0.rearrange("(p t) h -> p t h", t=NT)
+    c_ov = out_1.rearrange("(p t) h -> p t h", t=NT)
+    n_ov = out_2.rearrange("(p t) h -> p t h", t=NT)
+    m_ov = out_3.rearrange("(p t) h -> p t h", t=NT)
+
+    with tc.tile_pool(name="const", bufs=1) as const, tc.tile_pool(
+        name="xin", bufs=3
+    ) as xin, tc.tile_pool(name="state", bufs=4) as state, tc.tile_pool(
+        name="grp", bufs=2
+    ) as grp, tc.tile_pool(name="bl", bufs=2) as bl, tc.tile_pool(
+        name="al", bufs=2
+    ) as al, tc.tile_pool(name="outp", bufs=3) as outp, tc.tile_pool(
+        name="small", bufs=3
+    ) as small, tc.psum_pool(name="pxt", bufs=2) as pxt, tc.psum_pool(
+        name="pmx", bufs=3
+    ) as pmx, tc.psum_pool(name="pbk", bufs=3) as pbk:
+        warm = const.tile([P, 1], F32)
+        nc.vector.memset(warm[:], 0.0)
+        warm2 = const.tile([P, 1], F32)
+        nc.scalar.activation(out=warm2[:], in_=warm[:], func=ACT.Exp)
+
+        ident = const.tile([P, P], F32)
+        make_identity(nc, ident[:])
+        half = const.tile([P, TPC], F32)
+        nc.vector.memset(half[:], 0.5)
+
+        w_list = [wi_w, wf_w, wk_w[0], wq_w[0], wv_w[0], wo_w]
+        b_list = [wi_b, wf_b, wk_b, wv_b, wq_b, wo_b]
+        wraw = const.tile([P, 6, 4, H], BF16)
+        braw = const.tile([P, P], BF16)
+        nc.vector.memset(braw[:], 0.0)
+        wgrp = const.tile([P, 6, H, 4], BF16, align_bytes=64)
+        wcodes = const.tile([P, 6 * H], U32, align_bytes=64)
+        wscales = const.tile([P, 6 * H], U8, align_bytes=64)
+        bf32 = const.tile([P, P], F32)
+        bias = const.tile([P, 8], F32)
+        bks = const.tile([P, 1], F32)
+        boh = const.tile([P, 1], F32)
+
+        def load_bias(r):
+            nc.sync.dma_start(out=braw[r : r + 1, :], in_=b_list[r].unsqueeze(0))
+
+        def load_weight(g):
+            nc.sync.dma_start(
+                out=wraw[:, g, :, :].rearrange("p (u e) c -> p u e c", u=2),
+                in_=w_list[g].rearrange("(u q e) c -> q u e c", u=2, e=2),
+            )
+
+        def quantise_weights(g0, g1):
+            nc.vector.tensor_copy(
+                out=wgrp[:, g0:g1], in_=wraw[:, g0:g1].rearrange("p g t c -> p g c t")
+            )
+            nc.vector.quantize_mx(
+                out=wcodes[:, g0 * H : g1 * H].bitcast(FP8X4),
+                scales=wscales[:, g0 * H : g1 * H],
+                in_=wgrp[:, g0:g1].rearrange("p g c t -> p (g c t)"),
+            )
+
+        def spread_biases():
+            nc.vector.tensor_copy(out=bf32[:], in_=braw[:])
+            bps = pbk.tile([P, CW], F32, tag="bk", name="bps")
+            nc.tensor.transpose(bps[:, 0:P], bf32[:], ident[:])
+            nc.vector.tensor_copy(out=bias[:, 0:6], in_=bps[:, 0:6])
+            nc.vector.tensor_scalar_mul(out=bks[:], in0=bias[:, 2:3], scalar1=k_scale)
+            nc.vector.tensor_scalar_mul(out=boh[:], in0=bias[:, 5:6], scalar1=0.5)
+
+        st_tiles = {}
+
+        def load_x(x_view, c, nm):
+            xt_sb = xin.tile([P, TPC * K], BF16, tag="x" + nm, name="x" + nm)
+            nc.sync.dma_start(
+                out=xt_sb[:].rearrange("p (t k) -> p t k", t=TPC),
+                in_=x_view[:, c * TPC : (c + 1) * TPC, :],
+            )
+            return xt_sb
+
+        def quantise_x(xt_sb, nm):
+            xw = xt_sb[:].bitcast(F32)
+            grouped = grp.tile([P, 4 * CW], BF16, tag="g" + nm, name="g" + nm, align_bytes=64)
+            g32 = grouped[:].bitcast(F32)
+            for bnk in range(2):
+                xt = pxt.tile([P, CW], F32, tag="xt", name="xt")
+                for tt in range(2):
+                    t = 2 * bnk + tt
+                    for u in range(2):
+                        nc.tensor.transpose(
+                            xt[:, u * 256 + tt * P : u * 256 + (tt + 1) * P],
+                            xw[:, t * 256 + u * P : t * 256 + (u + 1) * P],
+                            ident[:],
+                        )
+                nc.scalar.copy(
+                    out=g32[:, bnk * CW : (bnk + 1) * CW].rearrange("p (b u) -> p b u", u=2),
+                    in_=xt[:].rearrange("p (u b) -> p b u", u=2),
+                )
+            codes = grp.tile([P, CW], U32, tag="c" + nm, name="c" + nm, align_bytes=64)
+            scales = grp.tile([P, CW], U8, tag="s" + nm, name="s" + nm, align_bytes=64)
+            nc.vector.quantize_mx(out=codes[:].bitcast(FP8X4), scales=scales[:], in_=grouped[:])
+            return codes, scales
+
+        def project(g, xq):
+            acc = pmx.tile([P, CW], F32, tag="mx", name="acc")
+            nc.tensor.matmul_mx(
+                out=acc[:],
+                lhsT=wcodes[:, g * H : (g + 1) * H].bitcast(FP8X4),
+                lhsT_scale=wscales[:, g * H : (g + 1) * H],
+                rhs=xq[0][:].bitcast(FP8X4),
+                rhs_scale=xq[1][:],
+                start=True,
+                stop=True,
+            )
+            return acc
+
+        def back(src, nm):
+            dst = pbk.tile([P, CW], F32, tag="bk", name="bk" + nm)
+            for t in range(TPC):
+                nc.tensor.transpose(dst[:, t * H : (t + 1) * H], src[:, t * P : (t + 1) * P], ident[:])
+            return dst
+
+        for r in range(3):
+            load_bias(r)
+        x_first = [load_x(xc_v, 0, "c")]
+        for r in range(3, 6):
+            load_bias(r)
+        for g in range(4):
+            load_weight(g)
+        x_first.append(load_x(xl_v, 0, "l"))
+        for g in range(4, 6):
+            load_weight(g)
+
+        for c in range(NCH):
+            if c % 2 == 0:
+                for nm, view in (("m", m_v), ("n", n_v), ("c", c_v)):
+                    st = state.tile([P, 2 * CW], BF16, tag="st" + nm, name="st" + nm)
+                    nc.sync.dma_start(
+                        out=st[:].rearrange("p (t h) -> p t h", h=H),
+                        in_=view[:, c * TPC : (c + 2) * TPC, :],
+                    )
+                    st_tiles[nm] = st
+            lo = (c % 2) * CW
+            m_in = st_tiles["m"][:, lo : lo + CW]
+            n_in = st_tiles["n"][:, lo : lo + CW]
+            c_in = st_tiles["c"][:, lo : lo + CW]
+
+            if c == 0:
+                xcq = quantise_x(x_first[0], "c")
+                spread_biases()
+                quantise_weights(0, 2)
+                quantise_weights(2, 4)
+                xlq = quantise_x(x_first[1], "l")
+                quantise_weights(4, 6)
+            else:
+                xcq = quantise_x(load_x(xc_v, c, "c"), "c")
+                xlq = quantise_x(load_x(xl_v, c, "l"), "l")
+
+            acc_i = project(0, xcq)
+            it_b = bl.tile([P, CW], F32, tag="it", name="it_b")
+            nc.scalar.activation(out=it_b[:], in_=acc_i[:], func=ACT.Identity, bias=bias[:, 0:1], scale=1.0)
+            acc_f = project(1, xcq)
+            tp_b = bl.tile([P, CW], F32, tag="tp", name="tp_b")
+            nc.vector.scalar_tensor_tensor(
+                out=tp_b[:], in0=acc_f[:], scalar=bias[:, 1:2], in1=it_b[:], op0=ALU.add, op1=ALU.subtract
+            )
+            acc_k = project(2, xcq)
+            k_b = bl.tile([P, CW], F32, tag="k", name="k_b")
+            nc.scalar.activation(out=k_b[:], in_=acc_k[:], func=ACT.Identity, bias=bks[:], scale=k_scale)
+            acc_v = project(4, xlq)
+            v_b = bl.tile([P, CW], F32, tag="v", name="v_b")
+            nc.scalar.activation(out=v_b[:], in_=acc_v[:], func=ACT.Identity, bias=bias[:, 3:4], scale=1.0)
+            acc_q = project(3, xcq)
+            q_b = bl.tile([P, CW], F32, tag="q", name="q_b")
+            nc.scalar.activation(out=q_b[:], in_=acc_q[:], func=ACT.Identity, bias=bias[:, 4:5], scale=1.0)
+            acc_o = project(5, xlq)
+            th_b = bl.tile([P, CW], F32, tag="th", name="th_b")
+            nc.scalar.activation(out=th_b[:], in_=acc_o[:], func=ACT.Tanh, bias=boh[:], scale=0.5)
+
+            tp_a = back(tp_b, "tp")
+            d = al.tile([P, CW], F32, tag="d", name="d")
+            nc.vector.tensor_tensor(out=d[:], in0=tp_a[:], in1=m_in, op=ALU.add)
+            e1 = al.tile([P, CW], F32, tag="e1", name="e1")
+            nc.scalar.activation(out=e1[:], in_=d[:], func=ACT.Exp, scale=-1.0)
+            e2 = al.tile([P, CW], F32, tag="e2", name="e2")
+            nc.scalar.activation(out=e2[:], in_=d[:], func=ACT.Exp, scale=1.0)
+            it_a = back(it_b, "it")
+            m_o = outp.tile([P, CW], F32, tag="mo", name="m_o")
+            nc.vector.scalar_tensor_tensor(
+                out=m_o[:], in0=d[:], scalar=0.0, in1=it_a[:], op0=ALU.max, op1=ALU.add
+            )
+            nc.sync.dma_start(
+                out=m_ov[:, c * TPC : (c + 1) * TPC, :], in_=m_o[:].rearrange("p (t h) -> p t h", h=H)
+            )
+            k_a = back(k_b, "k")
+            ik = al.tile([P, CW], F32, tag="ik", name="ik")
+            nc.vector.scalar_tensor_tensor(
+                out=ik[:], in0=e1[:], scalar=1.0, in1=k_a[:], op0=ALU.min, op1=ALU.mult
+            )
+            v_a = back(v_b, "v")
+            ikv = al.tile([P, CW], F32, tag="ikv", name="ikv")
+            nc.vector.tensor_tensor(out=ikv[:], in0=v_a[:], in1=ik[:], op=ALU.mult)
+            f_g = al.tile([P, CW], F32, tag="fg", name="f_g")
+            nc.gpsimd.tensor_scalar(
+                out=f_g[:], in0=e2[:], scalar1=1.0, scalar2=0.0, op0=ALU.min, op1=ALU.add
+            )
+            fn = al.tile([P, CW], F32, tag="fn", name="fn")
+            nc.gpsimd.tensor_tensor(out=fn[:], in0=f_g[:], in1=n_in, op=ALU.mult)
+            fc = al.tile([P, CW], F32, tag="fc", name="fc")
+            nc.gpsimd.tensor_tensor(out=fc[:], in0=f_g[:], in1=c_in, op=ALU.mult)
+            n_o = outp.tile([P, CW], F32, tag="no", name="n_o")
+            nc.vector.tensor_tensor(out=n_o[:], in0=fn[:], in1=ik[:], op=ALU.add)
+            nc.sync.dma_start(
+                out=n_ov[:, c * TPC : (c + 1) * TPC, :], in_=n_o[:].rearrange("p (t h) -> p t h", h=H)
+            )
+            c_o = outp.tile([P, CW], F32, tag="co", name="c_o")
+            nc.vector.tensor_tensor(out=c_o[:], in0=fc[:], in1=ikv[:], op=ALU.add)
+            nc.sync.dma_start(
+                out=c_ov[:, c * TPC : (c + 1) * TPC, :], in_=c_o[:].rearrange("p (t h) -> p t h", h=H)
+            )
+            q_a = back(q_b, "q")
+            nq = al.tile([P, CW], F32, tag="nq", name="nq")
+            nc.vector.tensor_tensor(out=nq[:], in0=q_a[:], in1=n_o[:], op=ALU.mult)
+            cq = al.tile([P, CW], F32, tag="cq", name="cq")
+            nc.vector.tensor_tensor(out=cq[:], in0=q_a[:], in1=c_o[:], op=ALU.mult)
+            sq = al.tile([P, CW], F32, tag="sq", name="sq")
+            ss = small.tile([P, TPC], F32, tag="ss", name="ss")
+            for t in range(TPC):
+                nc.scalar.activation(
+                    out=sq[:, t * H : (t + 1) * H],
+                    in_=nq[:, t * H : (t + 1) * H],
+                    func=ACT.Square,
+                    scale=2.0,
+                    accum_out=ss[:, t : t + 1],
+                )
+            th_a = back(th_b, "th")
+            h1 = al.tile([P, CW], F32, tag="h1", name="h1")
+            nc.vector.scalar_tensor_tensor(
+                out=h1[:], in0=th_a[:], scalar=1.0, in1=cq[:], op0=ALU.add, op1=ALU.mult
+            )
+            den = small.tile([P, TPC], F32, tag="den", name="den")
+            nc.gpsimd.tensor_tensor(out=den[:], in0=ss[:], in1=half[:], op=ALU.pow)
+            den2 = small.tile([P, TPC], F32, tag="den2", name="den2")
+            nc.vector.tensor_scalar_add(out=den2[:], in0=den[:], scalar1=2.0e-6)
+            rden = small.tile([P, TPC], F32, tag="rden", name="rden")
+            nc.vector.reciprocal(out=rden[:], in_=den2[:])
+            h_o = outp.tile([P, CW], F32, tag="ho", name="h_o")
+            for t in range(TPC):
+                nc.gpsimd.tensor_scalar(
+                    out=h_o[:, t * H : (t + 1) * H],
+                    in0=h1[:, t * H : (t + 1) * H],
+                    scalar1=rden[:, t : t + 1],
+                    scalar2=0.0,
+                    op0=ALU.mult,
+                    op1=ALU.add,
+                )
+            nc.sync.dma_start(
+                out=h_ov[:, c * TPC : (c + 1) * TPC, :], in_=h_o[:].rearrange("p (t h) -> p t h", h=H)
+            )

@@ -252,14 +252,14 @@ def tile_mlstmblock_pb_t_kernel(
             v_a = back(v_b, "v")
             ikv = al.tile([P, CW], F32, tag="ikv", name="ikv")
             nc.vector.tensor_tensor(out=ikv[:], in0=v_a[:], in1=ik[:], op=ALU.mult)
-            f_g = al.tile([P, CW], F32, tag="fg", name="f_g")
-            nc.gpsimd.tensor_scalar(
-                out=f_g[:], in0=e2[:], scalar1=1.0, scalar2=0.0, op0=ALU.min, op1=ALU.add
-            )
             fn = al.tile([P, CW], F32, tag="fn", name="fn")
-            nc.gpsimd.tensor_tensor(out=fn[:], in0=f_g[:], in1=n_in, op=ALU.mult)
+            nc.vector.scalar_tensor_tensor(
+                out=fn[:], in0=e2[:], scalar=1.0, in1=n_in, op0=ALU.min, op1=ALU.mult
+            )
             fc = al.tile([P, CW], F32, tag="fc", name="fc")
-            nc.gpsimd.tensor_tensor(out=fc[:], in0=f_g[:], in1=c_in, op=ALU.mult)
+            nc.vector.scalar_tensor_tensor(
+                out=fc[:], in0=e2[:], scalar=1.0, in1=c_in, op0=ALU.min, op1=ALU.mult
+            )
             n_o = outp.tile([P, CW], F32, tag="no", name="n_o")
             nc.vector.tensor_tensor(out=n_o[:], in0=fn[:], in1=ik[:], op=ALU.add)
             nc.sync.dma_start(

@@ -65,16 +65,17 @@ def tile_mlstmblock_pb_t_kernel(
         name="grp", bufs=2
     ) as grp, tc.tile_pool(name="bl", bufs=2) as bl, tc.tile_pool(
         name="al", bufs=2
-    ) as al, tc.tile_pool(name="outp", bufs=3) as outp, tc.tile_pool(
+    ) as al, tc.tile_pool(name="outp", bufs=2) as outp, tc.tile_pool(
         name="small", bufs=3
     ) as small, tc.psum_pool(name="pxt", bufs=2) as pxt, tc.psum_pool(
         name="pmx", bufs=3
-    ) as pmx, tc.psum_pool(name="pbk", bufs=3) as pbk:
+    ) as pmx, tc.psum_pool(name="pbk", bufs=3) as pbk, tc.manual_schedule():
+        live = {}
+
         warm = const.tile([P, 1], F32)
         nc.vector.memset(warm[:], 0.0)
         warm2 = const.tile([P, 1], F32)
         nc.scalar.activation(out=warm2[:], in_=warm[:], func=ACT.Exp)
-
         ident = const.tile([P, P], F32)
         make_identity(nc, ident[:])
         half = const.tile([P, TPC], F32)
@@ -112,200 +113,412 @@ def tile_mlstmblock_pb_t_kernel(
                 in_=wgrp[:, g0:g1].rearrange("p g c t -> p (g c t)"),
             )
 
-        def spread_biases():
-            nc.vector.tensor_copy(out=bf32[:], in_=braw[:])
-            bps = pbk.tile([P, CW], F32, tag="bk", name="bps")
-            nc.tensor.transpose(bps[:, 0:P], bf32[:], ident[:])
-            nc.vector.tensor_copy(out=bias[:, 0:6], in_=bps[:, 0:6])
-            nc.vector.tensor_scalar_mul(out=bks[:], in0=bias[:, 2:3], scalar1=k_scale)
-            nc.vector.tensor_scalar_mul(out=boh[:], in0=bias[:, 5:6], scalar1=0.5)
+        x_views = {"c": xc_v, "l": xl_v}
 
-        st_tiles = {}
+        def ld_x(c):
+            if c >= 2:
+                ld_x1(c, "c")
+                ld_x1(c, "l")
 
-        def load_x(x_view, c, nm):
+        def ld_x1(c, nm):
             xt_sb = xin.tile([P, TPC * K], BF16, tag="x" + nm, name="x" + nm)
             nc.sync.dma_start(
                 out=xt_sb[:].rearrange("p (t k) -> p t k", t=TPC),
-                in_=x_view[:, c * TPC : (c + 1) * TPC, :],
+                in_=x_views[nm][:, c * TPC : (c + 1) * TPC, :],
             )
-            return xt_sb
+            live[("x" + nm, c)] = xt_sb
 
-        def quantise_x(xt_sb, nm):
-            xw = xt_sb[:].bitcast(F32)
-            grouped = grp.tile([P, 4 * CW], BF16, tag="g" + nm, name="g" + nm, align_bytes=64)
-            g32 = grouped[:].bitcast(F32)
-            for bnk in range(2):
-                xt = pxt.tile([P, CW], F32, tag="xt", name="xt")
-                for tt in range(2):
-                    t = 2 * bnk + tt
-                    for u in range(2):
-                        nc.tensor.transpose(
-                            xt[:, u * 256 + tt * P : u * 256 + (tt + 1) * P],
-                            xw[:, t * 256 + u * P : t * 256 + (u + 1) * P],
-                            ident[:],
-                        )
-                nc.scalar.copy(
-                    out=g32[:, bnk * CW : (bnk + 1) * CW].rearrange("p (b u) -> p b u", u=2),
-                    in_=xt[:].rearrange("p (u b) -> p b u", u=2),
+        def ld_st(c):
+            if c >= 2 and c % 2 == 0:
+                ld_pair(c)
+
+        def ld_pair(c):
+            for nm, view in (("m", m_v), ("n", n_v), ("c", c_v)):
+                st = state.tile([P, 2 * CW], BF16, tag="st" + nm, name="st" + nm)
+                nc.sync.dma_start(
+                    out=st[:].rearrange("p (t h) -> p t h", h=H),
+                    in_=view[:, c * TPC : (c + 2) * TPC, :],
                 )
+                live[(nm + "in", c)] = st[:, 0:CW]
+                live[(nm + "in", c + 1)] = st[:, CW : 2 * CW]
+
+        def store(view, nm, c):
+            nc.sync.dma_start(
+                out=view[:, c * TPC : (c + 1) * TPC, :],
+                in_=live[(nm, c)][:].rearrange("p (t h) -> p t h", h=H),
+            )
+
+        def st_m(c):
+            store(m_ov, "m_o", c)
+
+        def st_n(c):
+            store(n_ov, "n_o", c)
+
+        def st_c(c):
+            store(c_ov, "c_o", c)
+
+        def st_h(c):
+            store(h_ov, "h_o", c)
+
+        def xt(c, nm, bnk):
+            xw = live[("x" + nm, c)][:].bitcast(F32)
+            bank = pxt.tile([P, CW], F32, tag="xt", name="xt")
+            for tt in range(2):
+                t = 2 * bnk + tt
+                for u in range(2):
+                    nc.tensor.transpose(
+                        bank[:, u * 256 + tt * P : u * 256 + (tt + 1) * P],
+                        xw[:, t * 256 + u * P : t * 256 + (u + 1) * P],
+                        ident[:],
+                    )
+            live[("xt" + nm, c, bnk)] = bank
+
+        def xe(c, nm, bnk):
+            if bnk == 0:
+                live[("g" + nm, c)] = grp.tile(
+                    [P, 4 * CW], BF16, tag="g" + nm, name="g" + nm, align_bytes=64
+                )
+            g32 = live[("g" + nm, c)][:].bitcast(F32)
+            nc.scalar.copy(
+                out=g32[:, bnk * CW : (bnk + 1) * CW].rearrange("p (b u) -> p b u", u=2),
+                in_=live[("xt" + nm, c, bnk)][:].rearrange("p (u b) -> p b u", u=2),
+            )
+
+        def qx(c, nm):
             codes = grp.tile([P, CW], U32, tag="c" + nm, name="c" + nm, align_bytes=64)
             scales = grp.tile([P, CW], U8, tag="s" + nm, name="s" + nm, align_bytes=64)
-            nc.vector.quantize_mx(out=codes[:].bitcast(FP8X4), scales=scales[:], in_=grouped[:])
-            return codes, scales
+            nc.vector.quantize_mx(
+                out=codes[:].bitcast(FP8X4), scales=scales[:], in_=live[("g" + nm, c)][:]
+            )
+            live[("q" + nm, c)] = (codes, scales)
 
-        def project(g, xq):
+        def xt_c0(c):
+            xt(c, "c", 0)
+
+        def xt_c1(c):
+            xt(c, "c", 1)
+            if c == 0:
+                bps = pbk.tile([P, CW], F32, tag="bk", name="bps")
+                nc.tensor.transpose(bps[:, 0:P], bf32[:], ident[:])
+                live["bps"] = bps
+
+        def xt_l0(c):
+            xt(c, "l", 0)
+
+        def xt_l1(c):
+            xt(c, "l", 1)
+
+        def xe_c0(c):
+            xe(c, "c", 0)
+
+        def xe_c1(c):
+            xe(c, "c", 1)
+
+        def xe_l0(c):
+            xe(c, "l", 0)
+
+        def xe_l1(c):
+            xe(c, "l", 1)
+
+        def qx_c(c):
+            if c == 0:
+                quantise_weights(0, 2)
+                nc.vector.tensor_copy(out=bias[:, 0:6], in_=live["bps"][:, 0:6])
+                nc.vector.tensor_scalar_mul(out=bks[:], in0=bias[:, 2:3], scalar1=k_scale)
+                nc.vector.tensor_scalar_mul(out=boh[:], in0=bias[:, 5:6], scalar1=0.5)
+            qx(c, "c")
+            if c == 0:
+                quantise_weights(2, 4)
+
+        def qx_l(c):
+            qx(c, "l")
+            if c == 0:
+                quantise_weights(4, 6)
+
+        def mx(c, g, nm, key):
+            codes, scales = live[("q" + nm, c)]
             acc = pmx.tile([P, CW], F32, tag="mx", name="acc")
             nc.tensor.matmul_mx(
                 out=acc[:],
                 lhsT=wcodes[:, g * H : (g + 1) * H].bitcast(FP8X4),
                 lhsT_scale=wscales[:, g * H : (g + 1) * H],
-                rhs=xq[0][:].bitcast(FP8X4),
-                rhs_scale=xq[1][:],
+                rhs=codes[:].bitcast(FP8X4),
+                rhs_scale=scales[:],
                 start=True,
                 stop=True,
             )
-            return acc
+            live[(key, c)] = acc
 
-        def back(src, nm):
-            dst = pbk.tile([P, CW], F32, tag="bk", name="bk" + nm)
+        def mx_i(c):
+            mx(c, 0, "c", "acc_i")
+
+        def mx_f(c):
+            mx(c, 1, "c", "acc_f")
+
+        def mx_k(c):
+            mx(c, 2, "c", "acc_k")
+
+        def mx_q(c):
+            mx(c, 3, "c", "acc_q")
+
+        def mx_v(c):
+            mx(c, 4, "l", "acc_v")
+
+        def mx_o(c):
+            mx(c, 5, "l", "acc_o")
+
+        def ev(c, key, func, b_ap, scale):
+            dst = bl.tile([P, CW], F32, tag=key, name=key + "_b")
+            nc.scalar.activation(
+                out=dst[:], in_=live[("acc_" + key, c)][:], func=func, bias=b_ap, scale=scale
+            )
+            live[(key + "_b", c)] = dst
+
+        def ev_i(c):
+            ev(c, "i", ACT.Identity, bias[:, 0:1], 1.0)
+
+        def ev_k(c):
+            ev(c, "k", ACT.Identity, bks[:], k_scale)
+
+        def ev_v(c):
+            ev(c, "v", ACT.Identity, bias[:, 3:4], 1.0)
+
+        def ev_q(c):
+            ev(c, "q", ACT.Identity, bias[:, 4:5], 1.0)
+
+        def ev_o(c):
+            ev(c, "o", ACT.Tanh, boh[:], 0.5)
+
+        def tp(c):
+            dst = bl.tile([P, CW], F32, tag="tp", name="tp_b")
+            nc.vector.scalar_tensor_tensor(
+                out=dst[:],
+                in0=live[("acc_f", c)][:],
+                scalar=bias[:, 1:2],
+                in1=live[("i_b", c)][:],
+                op0=ALU.add,
+                op1=ALU.subtract,
+            )
+            live[("tp_b", c)] = dst
+
+        def bt(c, key):
+            src = live[(key + "_b", c)]
+            dst = pbk.tile([P, CW], F32, tag="bk", name="bk" + key)
             for t in range(TPC):
-                nc.tensor.transpose(dst[:, t * H : (t + 1) * H], src[:, t * P : (t + 1) * P], ident[:])
-            return dst
+                nc.tensor.transpose(
+                    dst[:, t * H : (t + 1) * H], src[:, t * P : (t + 1) * P], ident[:]
+                )
+            live[(key + "_a", c)] = dst
 
-        for r in range(3):
-            load_bias(r)
-        x_first = [load_x(xc_v, 0, "c")]
-        for r in range(3, 6):
-            load_bias(r)
-        for g in range(4):
-            load_weight(g)
-        x_first.append(load_x(xl_v, 0, "l"))
-        for g in range(4, 6):
-            load_weight(g)
+        def bt_tp(c):
+            bt(c, "tp")
 
-        for c in range(NCH):
-            if c % 2 == 0:
-                for nm, view in (("m", m_v), ("n", n_v), ("c", c_v)):
-                    st = state.tile([P, 2 * CW], BF16, tag="st" + nm, name="st" + nm)
-                    nc.sync.dma_start(
-                        out=st[:].rearrange("p (t h) -> p t h", h=H),
-                        in_=view[:, c * TPC : (c + 2) * TPC, :],
-                    )
-                    st_tiles[nm] = st
-            lo = (c % 2) * CW
-            m_in = st_tiles["m"][:, lo : lo + CW]
-            n_in = st_tiles["n"][:, lo : lo + CW]
-            c_in = st_tiles["c"][:, lo : lo + CW]
+        def bt_i(c):
+            bt(c, "i")
 
-            if c == 0:
-                xcq = quantise_x(x_first[0], "c")
-                spread_biases()
-                quantise_weights(0, 2)
-                quantise_weights(2, 4)
-                xlq = quantise_x(x_first[1], "l")
-                quantise_weights(4, 6)
-            else:
-                xcq = quantise_x(load_x(xc_v, c, "c"), "c")
-                xlq = quantise_x(load_x(xl_v, c, "l"), "l")
+        def bt_k(c):
+            bt(c, "k")
 
-            acc_i = project(0, xcq)
-            it_b = bl.tile([P, CW], F32, tag="it", name="it_b")
-            nc.scalar.activation(out=it_b[:], in_=acc_i[:], func=ACT.Identity, bias=bias[:, 0:1], scale=1.0)
-            acc_f = project(1, xcq)
-            tp_b = bl.tile([P, CW], F32, tag="tp", name="tp_b")
-            nc.vector.scalar_tensor_tensor(
-                out=tp_b[:], in0=acc_f[:], scalar=bias[:, 1:2], in1=it_b[:], op0=ALU.add, op1=ALU.subtract
-            )
-            acc_k = project(2, xcq)
-            k_b = bl.tile([P, CW], F32, tag="k", name="k_b")
-            nc.scalar.activation(out=k_b[:], in_=acc_k[:], func=ACT.Identity, bias=bks[:], scale=k_scale)
-            acc_v = project(4, xlq)
-            v_b = bl.tile([P, CW], F32, tag="v", name="v_b")
-            nc.scalar.activation(out=v_b[:], in_=acc_v[:], func=ACT.Identity, bias=bias[:, 3:4], scale=1.0)
-            acc_q = project(3, xcq)
-            q_b = bl.tile([P, CW], F32, tag="q", name="q_b")
-            nc.scalar.activation(out=q_b[:], in_=acc_q[:], func=ACT.Identity, bias=bias[:, 4:5], scale=1.0)
-            acc_o = project(5, xlq)
-            th_b = bl.tile([P, CW], F32, tag="th", name="th_b")
-            nc.scalar.activation(out=th_b[:], in_=acc_o[:], func=ACT.Tanh, bias=boh[:], scale=0.5)
+        def bt_v(c):
+            bt(c, "v")
 
-            tp_a = back(tp_b, "tp")
-            d = al.tile([P, CW], F32, tag="d", name="d")
-            nc.vector.tensor_tensor(out=d[:], in0=tp_a[:], in1=m_in, op=ALU.add)
-            e1 = al.tile([P, CW], F32, tag="e1", name="e1")
-            nc.scalar.activation(out=e1[:], in_=d[:], func=ACT.Exp, scale=-1.0)
-            e2 = al.tile([P, CW], F32, tag="e2", name="e2")
-            nc.scalar.activation(out=e2[:], in_=d[:], func=ACT.Exp, scale=1.0)
-            it_a = back(it_b, "it")
-            m_o = outp.tile([P, CW], F32, tag="mo", name="m_o")
+        def bt_q(c):
+            bt(c, "q")
+
+        def bt_o(c):
+            bt(c, "o")
+
+        def new(pool, key, c):
+            t_new = pool.tile([P, CW], F32, tag=key, name=key)
+            live[(key, c)] = t_new
+            return t_new
+
+        def v_d(c):
+            nc.vector.tensor_tensor(
+                out=new(al, "d", c)[:], in0=live[("tp_a", c)][:], in1=live[("min", c)], op=ALU.add
+            )
+
+        def s_e1(c):
+            nc.scalar.activation(out=new(al, "e1", c)[:], in_=live[("d", c)][:], func=ACT.Exp, scale=-1.0)
+
+        def s_e2(c):
+            nc.scalar.activation(out=new(al, "e2", c)[:], in_=live[("d", c)][:], func=ACT.Exp, scale=1.0)
+
+        def v_m(c):
             nc.vector.scalar_tensor_tensor(
-                out=m_o[:], in0=d[:], scalar=0.0, in1=it_a[:], op0=ALU.max, op1=ALU.add
+                out=new(outp, "m_o", c)[:],
+                in0=live[("d", c)][:],
+                scalar=0.0,
+                in1=live[("i_a", c)][:],
+                op0=ALU.max,
+                op1=ALU.add,
             )
-            nc.sync.dma_start(
-                out=m_ov[:, c * TPC : (c + 1) * TPC, :], in_=m_o[:].rearrange("p (t h) -> p t h", h=H)
-            )
-            k_a = back(k_b, "k")
-            ik = al.tile([P, CW], F32, tag="ik", name="ik")
+
+        def v_ik(c):
             nc.vector.scalar_tensor_tensor(
-                out=ik[:], in0=e1[:], scalar=1.0, in1=k_a[:], op0=ALU.min, op1=ALU.mult
+                out=new(al, "ik", c)[:],
+                in0=live[("e1", c)][:],
+                scalar=1.0,
+                in1=live[("k_a", c)][:],
+                op0=ALU.min,
+                op1=ALU.mult,
             )
-            v_a = back(v_b, "v")
-            ikv = al.tile([P, CW], F32, tag="ikv", name="ikv")
-            nc.vector.tensor_tensor(out=ikv[:], in0=v_a[:], in1=ik[:], op=ALU.mult)
-            fn = al.tile([P, CW], F32, tag="fn", name="fn")
+
+        def v_fn(c):
             nc.vector.scalar_tensor_tensor(
-                out=fn[:], in0=e2[:], scalar=1.0, in1=n_in, op0=ALU.min, op1=ALU.mult
+                out=new(al, "fn", c)[:],
+                in0=live[("e2", c)][:],
+                scalar=1.0,
+                in1=live[("nin", c)],
+                op0=ALU.min,
+                op1=ALU.mult,
             )
-            fc = al.tile([P, CW], F32, tag="fc", name="fc")
+
+        def v_n(c):
+            nc.vector.tensor_tensor(
+                out=new(outp, "n_o", c)[:], in0=live[("fn", c)][:], in1=live[("ik", c)][:], op=ALU.add
+            )
+
+        def v_nq(c):
+            nc.vector.tensor_tensor(
+                out=new(al, "nq", c)[:], in0=live[("q_a", c)][:], in1=live[("n_o", c)][:], op=ALU.mult
+            )
+
+        def v_ikv(c):
+            nc.vector.tensor_tensor(
+                out=new(al, "ikv", c)[:], in0=live[("v_a", c)][:], in1=live[("ik", c)][:], op=ALU.mult
+            )
+
+        def v_fc(c):
             nc.vector.scalar_tensor_tensor(
-                out=fc[:], in0=e2[:], scalar=1.0, in1=c_in, op0=ALU.min, op1=ALU.mult
+                out=new(al, "fc", c)[:],
+                in0=live[("e2", c)][:],
+                scalar=1.0,
+                in1=live[("cin", c)],
+                op0=ALU.min,
+                op1=ALU.mult,
             )
-            n_o = outp.tile([P, CW], F32, tag="no", name="n_o")
-            nc.vector.tensor_tensor(out=n_o[:], in0=fn[:], in1=ik[:], op=ALU.add)
-            nc.sync.dma_start(
-                out=n_ov[:, c * TPC : (c + 1) * TPC, :], in_=n_o[:].rearrange("p (t h) -> p t h", h=H)
+
+        def v_c(c):
+            nc.vector.tensor_tensor(
+                out=new(outp, "c_o", c)[:], in0=live[("fc", c)][:], in1=live[("ikv", c)][:], op=ALU.add
             )
-            c_o = outp.tile([P, CW], F32, tag="co", name="c_o")
-            nc.vector.tensor_tensor(out=c_o[:], in0=fc[:], in1=ikv[:], op=ALU.add)
-            nc.sync.dma_start(
-                out=c_ov[:, c * TPC : (c + 1) * TPC, :], in_=c_o[:].rearrange("p (t h) -> p t h", h=H)
+
+        def v_cq(c):
+            nc.vector.tensor_tensor(
+                out=new(al, "cq", c)[:], in0=live[("q_a", c)][:], in1=live[("c_o", c)][:], op=ALU.mult
             )
-            q_a = back(q_b, "q")
-            nq = al.tile([P, CW], F32, tag="nq", name="nq")
-            nc.vector.tensor_tensor(out=nq[:], in0=q_a[:], in1=n_o[:], op=ALU.mult)
-            cq = al.tile([P, CW], F32, tag="cq", name="cq")
-            nc.vector.tensor_tensor(out=cq[:], in0=q_a[:], in1=c_o[:], op=ALU.mult)
+
+        def v_h1(c):
+            nc.vector.scalar_tensor_tensor(
+                out=new(al, "h1", c)[:],
+                in0=live[("o_a", c)][:],
+                scalar=1.0,
+                in1=live[("cq", c)][:],
+                op0=ALU.add,
+                op1=ALU.mult,
+            )
+
+        def s_sq(c):
             sq = al.tile([P, CW], F32, tag="sq", name="sq")
             ss = small.tile([P, TPC], F32, tag="ss", name="ss")
             for t in range(TPC):
                 nc.scalar.activation(
                     out=sq[:, t * H : (t + 1) * H],
-                    in_=nq[:, t * H : (t + 1) * H],
+                    in_=live[("nq", c)][:, t * H : (t + 1) * H],
                     func=ACT.Square,
                     scale=2.0,
                     accum_out=ss[:, t : t + 1],
                 )
-            th_a = back(th_b, "th")
-            h1 = al.tile([P, CW], F32, tag="h1", name="h1")
-            nc.vector.scalar_tensor_tensor(
-                out=h1[:], in0=th_a[:], scalar=1.0, in1=cq[:], op0=ALU.add, op1=ALU.mult
-            )
+            live[("ss", c)] = ss
+
+        def g_pow(c):
             den = small.tile([P, TPC], F32, tag="den", name="den")
-            nc.gpsimd.tensor_tensor(out=den[:], in0=ss[:], in1=half[:], op=ALU.pow)
+            nc.gpsimd.tensor_tensor(out=den[:], in0=live[("ss", c)][:], in1=half[:], op=ALU.pow)
+            live[("den", c)] = den
+
+        def v_hs(c):
             den2 = small.tile([P, TPC], F32, tag="den2", name="den2")
-            nc.vector.tensor_scalar_add(out=den2[:], in0=den[:], scalar1=2.0e-6)
+            nc.vector.tensor_scalar_add(out=den2[:], in0=live[("den", c)][:], scalar1=2.0e-6)
             rden = small.tile([P, TPC], F32, tag="rden", name="rden")
             nc.vector.reciprocal(out=rden[:], in_=den2[:])
-            h_o = outp.tile([P, CW], F32, tag="ho", name="h_o")
+            h_o = new(outp, "h_o", c)
             for t in range(TPC):
-                nc.gpsimd.tensor_scalar(
+                nc.vector.tensor_scalar_mul(
                     out=h_o[:, t * H : (t + 1) * H],
-                    in0=h1[:, t * H : (t + 1) * H],
+                    in0=live[("h1", c)][:, t * H : (t + 1) * H],
                     scalar1=rden[:, t : t + 1],
-                    scalar2=0.0,
-                    op0=ALU.mult,
-                    op1=ALU.add,
                 )
-            nc.sync.dma_start(
-                out=h_ov[:, c * TPC : (c + 1) * TPC, :], in_=h_o[:].rearrange("p (t h) -> p t h", h=H)
-            )
+
+        for r in range(3):
+            load_bias(r)
+        ld_x1(0, "c")
+        for r in range(3, 6):
+            load_bias(r)
+        for g in range(4):
+            load_weight(g)
+        ld_x1(0, "l")
+        for g in range(4, 6):
+            load_weight(g)
+        ld_pair(0)
+        ld_x1(1, "c")
+        ld_x1(1, "l")
+        nc.vector.tensor_copy(out=bf32[:], in_=braw[:])
+
+        period = [
+            (v_d, 0),
+            (ld_x, 5),
+            (ld_st, 4),
+            (v_m, 0),
+            (s_e1, 0),
+            (bt_v, 0),
+            (qx_c, 2),
+            (st_m, 0),
+            (s_e2, 0),
+            (bt_q, 0),
+            (mx_i, 1),
+            (mx_f, 1),
+            (mx_k, 1),
+            (qx_l, 2),
+            (ev_i, 1),
+            (v_hs, -1),
+            (ev_k, 1),
+            (mx_v, 1),
+            (tp, 1),
+            (st_h, -1),
+            (ev_v, 1),
+            (mx_q, 1),
+            (v_ik, 0),
+            (mx_o, 1),
+            (ev_q, 1),
+            (v_fn, 0),
+            (bt_o, 0),
+            (ev_o, 1),
+            (xt_c0, 3),
+            (xt_c1, 3),
+            (v_n, 0),
+            (xe_c0, 3),
+            (xe_c1, 3),
+            (v_nq, 0),
+            (st_n, 0),
+            (v_ikv, 0),
+            (s_sq, 0),
+            (xt_l0, 3),
+            (xt_l1, 3),
+            (v_fc, 0),
+            (bt_tp, 1),
+            (v_c, 0),
+            (xe_l0, 3),
+            (xe_l1, 3),
+            (g_pow, 0),
+            (v_cq, 0),
+            (st_c, 0),
+            (v_h1, 0),
+            (bt_i, 1),
+            (bt_k, 1),
+        ]
+        for n in range(-3, NCH + 1):
+            for step, lag in period:
+                c = n + lag
+                if 0 <= c < NCH:
+                    step(c)

@@ -65,17 +65,16 @@ def tile_mlstmblock_pb_t_kernel(
         name="grp", bufs=2
     ) as grp, tc.tile_pool(name="bl", bufs=2) as bl, tc.tile_pool(
         name="al", bufs=2
-    ) as al, tc.tile_pool(name="outp", bufs=2) as outp, tc.tile_pool(
+    ) as al, tc.tile_pool(name="outp", bufs=3) as outp, tc.tile_pool(
         name="small", bufs=3
     ) as small, tc.psum_pool(name="pxt", bufs=2) as pxt, tc.psum_pool(
         name="pmx", bufs=3
-    ) as pmx, tc.psum_pool(name="pbk", bufs=3) as pbk, tc.manual_schedule():
-        live = {}
-
+    ) as pmx, tc.psum_pool(name="pbk", bufs=3) as pbk:
         warm = const.tile([P, 1], F32)
         nc.vector.memset(warm[:], 0.0)
         warm2 = const.tile([P, 1], F32)
         nc.scalar.activation(out=warm2[:], in_=warm[:], func=ACT.Exp)
+
         ident = const.tile([P, P], F32)
         make_identity(nc, ident[:])
         half = const.tile([P, TPC], F32)
@@ -113,412 +112,211 @@ def tile_mlstmblock_pb_t_kernel(
                 in_=wgrp[:, g0:g1].rearrange("p g c t -> p (g c t)"),
             )
 
-        x_views = {"c": xc_v, "l": xl_v}
+        def spread_biases():
+            nc.vector.tensor_copy(out=bf32[:], in_=braw[:])
+            bps = pbk.tile([P, CW], F32, tag="bk", name="bps")
+            nc.tensor.transpose(bps[:, 0:P], bf32[:], ident[:])
+            nc.vector.tensor_copy(out=bias[:, 0:6], in_=bps[:, 0:6])
+            nc.vector.tensor_scalar_mul(out=bks[:], in0=bias[:, 2:3], scalar1=k_scale)
+            nc.vector.tensor_scalar_mul(out=boh[:], in0=bias[:, 5:6], scalar1=0.5)
 
-        def ld_x(c):
-            if c >= 2:
-                ld_x1(c, "c")
-                ld_x1(c, "l")
+        st_tiles = {}
 
-        def ld_x1(c, nm):
+        def load_x(x_view, c, nm):
             xt_sb = xin.tile([P, TPC * K], BF16, tag="x" + nm, name="x" + nm)
             nc.sync.dma_start(
                 out=xt_sb[:].rearrange("p (t k) -> p t k", t=TPC),
-                in_=x_views[nm][:, c * TPC : (c + 1) * TPC, :],
+                in_=x_view[:, c * TPC : (c + 1) * TPC, :],
             )
-            live[("x" + nm, c)] = xt_sb
+            return xt_sb
 
-        def ld_st(c):
-            if c >= 2 and c % 2 == 0:
-                ld_pair(c)
-
-        def ld_pair(c):
-            for nm, view in (("m", m_v), ("n", n_v), ("c", c_v)):
-                st = state.tile([P, 2 * CW], BF16, tag="st" + nm, name="st" + nm)
-                nc.sync.dma_start(
-                    out=st[:].rearrange("p (t h) -> p t h", h=H),
-                    in_=view[:, c * TPC : (c + 2) * TPC, :],
+        def quantise_x(xt_sb, nm):
+            xw = xt_sb[:].bitcast(F32)
+            grouped = grp.tile([P, 4 * CW], BF16, tag="g" + nm, name="g" + nm, align_bytes=64)
+            g32 = grouped[:].bitcast(F32)
+            for bnk in range(2):
+                xt = pxt.tile([P, CW], F32, tag="xt", name="xt")
+                for tt in range(2):
+                    t = 2 * bnk + tt
+                    for u in range(2):
+                        nc.tensor.transpose(
+                            xt[:, u * 256 + tt * P : u * 256 + (tt + 1) * P],
+                            xw[:, t * 256 + u * P : t * 256 + (u + 1) * P],
+                            ident[:],
+                        )
+                nc.scalar.copy(
+                    out=g32[:, bnk * CW : (bnk + 1) * CW].rearrange("p (b u) -> p b u", u=2),
+                    in_=xt[:].rearrange("p (u b) -> p b u", u=2),
                 )
-                live[(nm + "in", c)] = st[:, 0:CW]
-                live[(nm + "in", c + 1)] = st[:, CW : 2 * CW]
-
-        def store(view, nm, c):
-            nc.sync.dma_start(
-                out=view[:, c * TPC : (c + 1) * TPC, :],
-                in_=live[(nm, c)][:].rearrange("p (t h) -> p t h", h=H),
-            )
-
-        def st_m(c):
-            store(m_ov, "m_o", c)
-
-        def st_n(c):
-            store(n_ov, "n_o", c)
-
-        def st_c(c):
-            store(c_ov, "c_o", c)
-
-        def st_h(c):
-            store(h_ov, "h_o", c)
-
-        def xt(c, nm, bnk):
-            xw = live[("x" + nm, c)][:].bitcast(F32)
-            bank = pxt.tile([P, CW], F32, tag="xt", name="xt")
-            for tt in range(2):
-                t = 2 * bnk + tt
-                for u in range(2):
-                    nc.tensor.transpose(
-                        bank[:, u * 256 + tt * P : u * 256 + (tt + 1) * P],
-                        xw[:, t * 256 + u * P : t * 256 + (u + 1) * P],
-                        ident[:],
-                    )
-            live[("xt" + nm, c, bnk)] = bank
-
-        def xe(c, nm, bnk):
-            if bnk == 0:
-                live[("g" + nm, c)] = grp.tile(
-                    [P, 4 * CW], BF16, tag="g" + nm, name="g" + nm, align_bytes=64
-                )
-            g32 = live[("g" + nm, c)][:].bitcast(F32)
-            nc.scalar.copy(
-                out=g32[:, bnk * CW : (bnk + 1) * CW].rearrange("p (b u) -> p b u", u=2),
-                in_=live[("xt" + nm, c, bnk)][:].rearrange("p (u b) -> p b u", u=2),
-            )
-
-        def qx(c, nm):
             codes = grp.tile([P, CW], U32, tag="c" + nm, name="c" + nm, align_bytes=64)
             scales = grp.tile([P, CW], U8, tag="s" + nm, name="s" + nm, align_bytes=64)
-            nc.vector.quantize_mx(
-                out=codes[:].bitcast(FP8X4), scales=scales[:], in_=live[("g" + nm, c)][:]
-            )
-            live[("q" + nm, c)] = (codes, scales)
+            nc.vector.quantize_mx(out=codes[:].bitcast(FP8X4), scales=scales[:], in_=grouped[:])
+            return codes, scales
 
-        def xt_c0(c):
-            xt(c, "c", 0)
-
-        def xt_c1(c):
-            xt(c, "c", 1)
-            if c == 0:
-                bps = pbk.tile([P, CW], F32, tag="bk", name="bps")
-                nc.tensor.transpose(bps[:, 0:P], bf32[:], ident[:])
-                live["bps"] = bps
-
-        def xt_l0(c):
-            xt(c, "l", 0)
-
-        def xt_l1(c):
-            xt(c, "l", 1)
-
-        def xe_c0(c):
-            xe(c, "c", 0)
-
-        def xe_c1(c):
-            xe(c, "c", 1)
-
-        def xe_l0(c):
-            xe(c, "l", 0)
-
-        def xe_l1(c):
-            xe(c, "l", 1)
-
-        def qx_c(c):
-            if c == 0:
-                quantise_weights(0, 2)
-                nc.vector.tensor_copy(out=bias[:, 0:6], in_=live["bps"][:, 0:6])
-                nc.vector.tensor_scalar_mul(out=bks[:], in0=bias[:, 2:3], scalar1=k_scale)
-                nc.vector.tensor_scalar_mul(out=boh[:], in0=bias[:, 5:6], scalar1=0.5)
-            qx(c, "c")
-            if c == 0:
-                quantise_weights(2, 4)
-
-        def qx_l(c):
-            qx(c, "l")
-            if c == 0:
-                quantise_weights(4, 6)
-
-        def mx(c, g, nm, key):
-            codes, scales = live[("q" + nm, c)]
+        def project(g, xq):
             acc = pmx.tile([P, CW], F32, tag="mx", name="acc")
             nc.tensor.matmul_mx(
                 out=acc[:],
                 lhsT=wcodes[:, g * H : (g + 1) * H].bitcast(FP8X4),
                 lhsT_scale=wscales[:, g * H : (g + 1) * H],
-                rhs=codes[:].bitcast(FP8X4),
-                rhs_scale=scales[:],
+                rhs=xq[0][:].bitcast(FP8X4),
+                rhs_scale=xq[1][:],
                 start=True,
                 stop=True,
             )
-            live[(key, c)] = acc
+            return acc
 
-        def mx_i(c):
-            mx(c, 0, "c", "acc_i")
-
-        def mx_f(c):
-            mx(c, 1, "c", "acc_f")
-
-        def mx_k(c):
-            mx(c, 2, "c", "acc_k")
-
-        def mx_q(c):
-            mx(c, 3, "c", "acc_q")
-
-        def mx_v(c):
-            mx(c, 4, "l", "acc_v")
-
-        def mx_o(c):
-            mx(c, 5, "l", "acc_o")
-
-        def ev(c, key, func, b_ap, scale):
-            dst = bl.tile([P, CW], F32, tag=key, name=key + "_b")
-            nc.scalar.activation(
-                out=dst[:], in_=live[("acc_" + key, c)][:], func=func, bias=b_ap, scale=scale
-            )
-            live[(key + "_b", c)] = dst
-
-        def ev_i(c):
-            ev(c, "i", ACT.Identity, bias[:, 0:1], 1.0)
-
-        def ev_k(c):
-            ev(c, "k", ACT.Identity, bks[:], k_scale)
-
-        def ev_v(c):
-            ev(c, "v", ACT.Identity, bias[:, 3:4], 1.0)
-
-        def ev_q(c):
-            ev(c, "q", ACT.Identity, bias[:, 4:5], 1.0)
-
-        def ev_o(c):
-            ev(c, "o", ACT.Tanh, boh[:], 0.5)
-
-        def tp(c):
-            dst = bl.tile([P, CW], F32, tag="tp", name="tp_b")
-            nc.vector.scalar_tensor_tensor(
-                out=dst[:],
-                in0=live[("acc_f", c)][:],
-                scalar=bias[:, 1:2],
-                in1=live[("i_b", c)][:],
-                op0=ALU.add,
-                op1=ALU.subtract,
-            )
-            live[("tp_b", c)] = dst
-
-        def bt(c, key):
-            src = live[(key + "_b", c)]
-            dst = pbk.tile([P, CW], F32, tag="bk", name="bk" + key)
+        def back(src, nm):
+            dst = pbk.tile([P, CW], F32, tag="bk", name="bk" + nm)
+            if nm in ("tp", "k", "q"):
+                for rep in range(2):
+                    nc.tensor.matmul_mx(
+                        out=dst[:],
+                        lhsT=wcodes[:, 0:H].bitcast(FP8X4),
+                        lhsT_scale=wscales[:, 0:H],
+                        rhs=wcodes[:, 0:CW].bitcast(FP8X4),
+                        rhs_scale=wscales[:, 0:CW],
+                        start=True,
+                        stop=True,
+                    )
             for t in range(TPC):
-                nc.tensor.transpose(
-                    dst[:, t * H : (t + 1) * H], src[:, t * P : (t + 1) * P], ident[:]
-                )
-            live[(key + "_a", c)] = dst
+                nc.tensor.transpose(dst[:, t * H : (t + 1) * H], src[:, t * P : (t + 1) * P], ident[:])
+            return dst
 
-        def bt_tp(c):
-            bt(c, "tp")
+        for r in range(3):
+            load_bias(r)
+        x_first = [load_x(xc_v, 0, "c")]
+        for r in range(3, 6):
+            load_bias(r)
+        for g in range(4):
+            load_weight(g)
+        x_first.append(load_x(xl_v, 0, "l"))
+        for g in range(4, 6):
+            load_weight(g)
 
-        def bt_i(c):
-            bt(c, "i")
+        for c in range(NCH):
+            if c % 2 == 0:
+                for nm, view in (("m", m_v), ("n", n_v), ("c", c_v)):
+                    st = state.tile([P, 2 * CW], BF16, tag="st" + nm, name="st" + nm)
+                    nc.sync.dma_start(
+                        out=st[:].rearrange("p (t h) -> p t h", h=H),
+                        in_=view[:, c * TPC : (c + 2) * TPC, :],
+                    )
+                    st_tiles[nm] = st
+            lo = (c % 2) * CW
+            m_in = st_tiles["m"][:, lo : lo + CW]
+            n_in = st_tiles["n"][:, lo : lo + CW]
+            c_in = st_tiles["c"][:, lo : lo + CW]
 
-        def bt_k(c):
-            bt(c, "k")
+            if c == 0:
+                xcq = quantise_x(x_first[0], "c")
+                spread_biases()
+                quantise_weights(0, 2)
+                quantise_weights(2, 4)
+                xlq = quantise_x(x_first[1], "l")
+                quantise_weights(4, 6)
+            else:
+                xcq = quantise_x(load_x(xc_v, c, "c"), "c")
+                xlq = quantise_x(load_x(xl_v, c, "l"), "l")
 
-        def bt_v(c):
-            bt(c, "v")
-
-        def bt_q(c):
-            bt(c, "q")
-
-        def bt_o(c):
-            bt(c, "o")
-
-        def new(pool, key, c):
-            t_new = pool.tile([P, CW], F32, tag=key, name=key)
-            live[(key, c)] = t_new
-            return t_new
-
-        def v_d(c):
-            nc.vector.tensor_tensor(
-                out=new(al, "d", c)[:], in0=live[("tp_a", c)][:], in1=live[("min", c)], op=ALU.add
-            )
-
-        def s_e1(c):
-            nc.scalar.activation(out=new(al, "e1", c)[:], in_=live[("d", c)][:], func=ACT.Exp, scale=-1.0)
-
-        def s_e2(c):
-            nc.scalar.activation(out=new(al, "e2", c)[:], in_=live[("d", c)][:], func=ACT.Exp, scale=1.0)
-
-        def v_m(c):
+            acc_i = project(0, xcq)
+            it_b = bl.tile([P, CW], F32, tag="it", name="it_b")
+            nc.scalar.activation(out=it_b[:], in_=acc_i[:], func=ACT.Identity, bias=bias[:, 0:1], scale=1.0)
+            acc_f = project(1, xcq)
+            tp_b = bl.tile([P, CW], F32, tag="tp", name="tp_b")
             nc.vector.scalar_tensor_tensor(
-                out=new(outp, "m_o", c)[:],
-                in0=live[("d", c)][:],
-                scalar=0.0,
-                in1=live[("i_a", c)][:],
-                op0=ALU.max,
-                op1=ALU.add,
+                out=tp_b[:], in0=acc_f[:], scalar=bias[:, 1:2], in1=it_b[:], op0=ALU.add, op1=ALU.subtract
             )
+            acc_k = project(2, xcq)
+            k_b = bl.tile([P, CW], F32, tag="k", name="k_b")
+            nc.scalar.activation(out=k_b[:], in_=acc_k[:], func=ACT.Identity, bias=bks[:], scale=k_scale)
+            acc_v = project(4, xlq)
+            v_b = bl.tile([P, CW], F32, tag="v", name="v_b")
+            nc.scalar.activation(out=v_b[:], in_=acc_v[:], func=ACT.Identity, bias=bias[:, 3:4], scale=1.0)
+            acc_q = project(3, xcq)
+            q_b = bl.tile([P, CW], F32, tag="q", name="q_b")
+            nc.scalar.activation(out=q_b[:], in_=acc_q[:], func=ACT.Identity, bias=bias[:, 4:5], scale=1.0)
+            acc_o = project(5, xlq)
+            th_b = bl.tile([P, CW], F32, tag="th", name="th_b")
+            nc.scalar.activation(out=th_b[:], in_=acc_o[:], func=ACT.Tanh, bias=boh[:], scale=0.5)
 
-        def v_ik(c):
+            tp_a = back(tp_b, "tp")
+            d = al.tile([P, CW], F32, tag="d", name="d")
+            nc.vector.tensor_tensor(out=d[:], in0=tp_a[:], in1=m_in, op=ALU.add)
+            e1 = al.tile([P, CW], F32, tag="e1", name="e1")
+            nc.scalar.activation(out=e1[:], in_=d[:], func=ACT.Exp, scale=-1.0)
+            e2 = al.tile([P, CW], F32, tag="e2", name="e2")
+            nc.scalar.activation(out=e2[:], in_=d[:], func=ACT.Exp, scale=1.0)
+            it_a = back(it_b, "it")
+            m_o = outp.tile([P, CW], F32, tag="mo", name="m_o")
             nc.vector.scalar_tensor_tensor(
-                out=new(al, "ik", c)[:],
-                in0=live[("e1", c)][:],
-                scalar=1.0,
-                in1=live[("k_a", c)][:],
-                op0=ALU.min,
-                op1=ALU.mult,
+                out=m_o[:], in0=d[:], scalar=0.0, in1=it_a[:], op0=ALU.max, op1=ALU.add
             )
-
-        def v_fn(c):
+            nc.sync.dma_start(
+                out=m_ov[:, c * TPC : (c + 1) * TPC, :], in_=m_o[:].rearrange("p (t h) -> p t h", h=H)
+            )
+            k_a = back(k_b, "k")
+            ik = al.tile([P, CW], F32, tag="ik", name="ik")
             nc.vector.scalar_tensor_tensor(
-                out=new(al, "fn", c)[:],
-                in0=live[("e2", c)][:],
-                scalar=1.0,
-                in1=live[("nin", c)],
-                op0=ALU.min,
-                op1=ALU.mult,
+                out=ik[:], in0=e1[:], scalar=1.0, in1=k_a[:], op0=ALU.min, op1=ALU.mult
             )
-
-        def v_n(c):
-            nc.vector.tensor_tensor(
-                out=new(outp, "n_o", c)[:], in0=live[("fn", c)][:], in1=live[("ik", c)][:], op=ALU.add
-            )
-
-        def v_nq(c):
-            nc.vector.tensor_tensor(
-                out=new(al, "nq", c)[:], in0=live[("q_a", c)][:], in1=live[("n_o", c)][:], op=ALU.mult
-            )
-
-        def v_ikv(c):
-            nc.vector.tensor_tensor(
-                out=new(al, "ikv", c)[:], in0=live[("v_a", c)][:], in1=live[("ik", c)][:], op=ALU.mult
-            )
-
-        def v_fc(c):
+            v_a = back(v_b, "v")
+            ikv = al.tile([P, CW], F32, tag="ikv", name="ikv")
+            nc.vector.tensor_tensor(out=ikv[:], in0=v_a[:], in1=ik[:], op=ALU.mult)
+            fn = al.tile([P, CW], F32, tag="fn", name="fn")
             nc.vector.scalar_tensor_tensor(
-                out=new(al, "fc", c)[:],
-                in0=live[("e2", c)][:],
-                scalar=1.0,
-                in1=live[("cin", c)],
-                op0=ALU.min,
-                op1=ALU.mult,
+                out=fn[:], in0=e2[:], scalar=1.0, in1=n_in, op0=ALU.min, op1=ALU.mult
             )
-
-        def v_c(c):
-            nc.vector.tensor_tensor(
-                out=new(outp, "c_o", c)[:], in0=live[("fc", c)][:], in1=live[("ikv", c)][:], op=ALU.add
-            )
-
-        def v_cq(c):
-            nc.vector.tensor_tensor(
-                out=new(al, "cq", c)[:], in0=live[("q_a", c)][:], in1=live[("c_o", c)][:], op=ALU.mult
-            )
-
-        def v_h1(c):
+            fc = al.tile([P, CW], F32, tag="fc", name="fc")
             nc.vector.scalar_tensor_tensor(
-                out=new(al, "h1", c)[:],
-                in0=live[("o_a", c)][:],
-                scalar=1.0,
-                in1=live[("cq", c)][:],
-                op0=ALU.add,
-                op1=ALU.mult,
+                out=fc[:], in0=e2[:], scalar=1.0, in1=c_in, op0=ALU.min, op1=ALU.mult
             )
-
-        def s_sq(c):
+            n_o = outp.tile([P, CW], F32, tag="no", name="n_o")
+            nc.vector.tensor_tensor(out=n_o[:], in0=fn[:], in1=ik[:], op=ALU.add)
+            nc.sync.dma_start(
+                out=n_ov[:, c * TPC : (c + 1) * TPC, :], in_=n_o[:].rearrange("p (t h) -> p t h", h=H)
+            )
+            c_o = outp.tile([P, CW], F32, tag="co", name="c_o")
+            nc.vector.tensor_tensor(out=c_o[:], in0=fc[:], in1=ikv[:], op=ALU.add)
+            nc.sync.dma_start(
+                out=c_ov[:, c * TPC : (c + 1) * TPC, :], in_=c_o[:].rearrange("p (t h) -> p t h", h=H)
+            )
+            q_a = back(q_b, "q")
+            nq = al.tile([P, CW], F32, tag="nq", name="nq")
+            nc.vector.tensor_tensor(out=nq[:], in0=q_a[:], in1=n_o[:], op=ALU.mult)
+            cq = al.tile([P, CW], F32, tag="cq", name="cq")
+            nc.vector.tensor_tensor(out=cq[:], in0=q_a[:], in1=c_o[:], op=ALU.mult)
             sq = al.tile([P, CW], F32, tag="sq", name="sq")
             ss = small.tile([P, TPC], F32, tag="ss", name="ss")
             for t in range(TPC):
                 nc.scalar.activation(
                     out=sq[:, t * H : (t + 1) * H],
-                    in_=live[("nq", c)][:, t * H : (t + 1) * H],
+                    in_=nq[:, t * H : (t + 1) * H],
                     func=ACT.Square,
                     scale=2.0,
                     accum_out=ss[:, t : t + 1],
                 )
-            live[("ss", c)] = ss
-
-        def g_pow(c):
+            th_a = back(th_b, "th")
+            h1 = al.tile([P, CW], F32, tag="h1", name="h1")
+            nc.vector.scalar_tensor_tensor(
+                out=h1[:], in0=th_a[:], scalar=1.0, in1=cq[:], op0=ALU.add, op1=ALU.mult
+            )
             den = small.tile([P, TPC], F32, tag="den", name="den")
-            nc.gpsimd.tensor_tensor(out=den[:], in0=live[("ss", c)][:], in1=half[:], op=ALU.pow)
-            live[("den", c)] = den
-
-        def v_hs(c):
+            nc.gpsimd.tensor_tensor(out=den[:], in0=ss[:], in1=half[:], op=ALU.pow)
             den2 = small.tile([P, TPC], F32, tag="den2", name="den2")
-            nc.vector.tensor_scalar_add(out=den2[:], in0=live[("den", c)][:], scalar1=2.0e-6)
+            nc.vector.tensor_scalar_add(out=den2[:], in0=den[:], scalar1=2.0e-6)
             rden = small.tile([P, TPC], F32, tag="rden", name="rden")
             nc.vector.reciprocal(out=rden[:], in_=den2[:])
-            h_o = new(outp, "h_o", c)
+            h_o = outp.tile([P, CW], F32, tag="ho", name="h_o")
             for t in range(TPC):
-                nc.vector.tensor_scalar_mul(
+                nc.gpsimd.tensor_scalar(
                     out=h_o[:, t * H : (t + 1) * H],
-                    in0=live[("h1", c)][:, t * H : (t + 1) * H],
+                    in0=h1[:, t * H : (t + 1) * H],
                     scalar1=rden[:, t : t + 1],
+                    scalar2=0.0,
+                    op0=ALU.mult,
+                    op1=ALU.add,
                 )
-
-        for r in range(3):
-            load_bias(r)
-        ld_x1(0, "c")
-        for r in range(3, 6):
-            load_bias(r)
-        for g in range(4):
-            load_weight(g)
-        ld_x1(0, "l")
-        for g in range(4, 6):
-            load_weight(g)
-        ld_pair(0)
-        ld_x1(1, "c")
-        ld_x1(1, "l")
-        nc.vector.tensor_copy(out=bf32[:], in_=braw[:])
-
-        period = [
-            (v_d, 0),
-            (ld_x, 5),
-            (ld_st, 4),
-            (v_m, 0),
-            (s_e1, 0),
-            (bt_v, 0),
-            (qx_c, 2),
-            (st_m, 0),
-            (s_e2, 0),
-            (bt_q, 0),
-            (mx_i, 1),
-            (mx_f, 1),
-            (mx_k, 1),
-            (qx_l, 2),
-            (ev_i, 1),
-            (v_hs, -1),
-            (ev_k, 1),
-            (mx_v, 1),
-            (tp, 1),
-            (st_h, -1),
-            (ev_v, 1),
-            (mx_q, 1),
-            (v_ik, 0),
-            (mx_o, 1),
-            (ev_q, 1),
-            (v_fn, 0),
-            (bt_o, 0),
-            (ev_o, 1),
-            (xt_c0, 3),
-            (xt_c1, 3),
-            (v_n, 0),
-            (xe_c0, 3),
-            (xe_c1, 3),
-            (v_nq, 0),
-            (st_n, 0),
-            (v_ikv, 0),
-            (s_sq, 0),
-            (xt_l0, 3),
-            (xt_l1, 3),
-            (v_fc, 0),
-            (bt_tp, 1),
-            (v_c, 0),
-            (xe_l0, 3),
-            (xe_l1, 3),
-            (g_pow, 0),
-            (v_cq, 0),
-            (st_c, 0),
-            (v_h1, 0),
-            (bt_i, 1),
-            (bt_k, 1),
-        ]
-        for n in range(-3, NCH + 1):
-            for step, lag in period:
-                c = n + lag
-                if 0 <= c < NCH:
-                    step(c)
+            nc.sync.dma_start(
+                out=h_ov[:, c * TPC : (c + 1) * TPC, :], in_=h_o[:].rearrange("p (t h) -> p t h", h=H)
+            )

@@ -12,14 +12,16 @@ ALU = mybir.AluOpType
 ACT = mybir.ActivationFunctionType
 
 P = 128
-B = 4096
+ROWS = 4096
 K = 512
 H = 128
-NT = B // P
+TILES = ROWS // P
 TPC = 4
-NCH = NT // TPC
+CHUNKS = TILES // TPC
 CW = TPC * H
-FLOPS = 2 * B * K * H * 6
+GATES = 6
+G_I, G_F, G_K, G_Q, G_V, G_O = 0, 1, 2, 3, 4, 5
+FLOPS = 2 * ROWS * K * H * GATES
 
 
 def tile_mlstmblock_pb_t_kernel(
@@ -49,274 +51,366 @@ def tile_mlstmblock_pb_t_kernel(
     nc = tc.nc
     k_scale = 1.0 / math.sqrt(float(H))
 
-    xc_v = x_conv.rearrange("(p t) k -> p t k", t=NT)
-    xl_v = x_left.rearrange("(p t) k -> p t k", t=NT)
-    c_v = c_prev.rearrange("(p t) h -> p t h", t=NT)
-    n_v = n_prev.rearrange("(p t) h -> p t h", t=NT)
-    m_v = m_prev.rearrange("(p t) h -> p t h", t=NT)
-    h_ov = out_0.rearrange("(p t) h -> p t h", t=NT)
-    c_ov = out_1.rearrange("(p t) h -> p t h", t=NT)
-    n_ov = out_2.rearrange("(p t) h -> p t h", t=NT)
-    m_ov = out_3.rearrange("(p t) h -> p t h", t=NT)
+    def by_partition(dram):
+        return dram.rearrange("(p t) w -> p t w", t=TILES)
+
+    x_views = {"c": by_partition(x_conv), "l": by_partition(x_left)}
+    state_views = {"m": by_partition(m_prev), "n": by_partition(n_prev), "c": by_partition(c_prev)}
+    out_views = {
+        "h": by_partition(out_0),
+        "c": by_partition(out_1),
+        "n": by_partition(out_2),
+        "m": by_partition(out_3),
+    }
+    weights = [None] * GATES
+    biases = [None] * GATES
+    for g, w_ap, b_ap in (
+        (G_I, wi_w, wi_b),
+        (G_F, wf_w, wf_b),
+        (G_K, wk_w[0], wk_b),
+        (G_Q, wq_w[0], wq_b),
+        (G_V, wv_w[0], wv_b),
+        (G_O, wo_w, wo_b),
+    ):
+        weights[g] = w_ap
+        biases[g] = b_ap
 
     with tc.tile_pool(name="const", bufs=1) as const, tc.tile_pool(
         name="xin", bufs=3
-    ) as xin, tc.tile_pool(name="state", bufs=4) as state, tc.tile_pool(
-        name="grp", bufs=2
-    ) as grp, tc.tile_pool(name="bl", bufs=2) as bl, tc.tile_pool(
-        name="al", bufs=2
-    ) as al, tc.tile_pool(name="outp", bufs=3) as outp, tc.tile_pool(
-        name="small", bufs=3
-    ) as small, tc.psum_pool(name="pxt", bufs=2) as pxt, tc.psum_pool(
-        name="pmx", bufs=3
-    ) as pmx, tc.psum_pool(name="pbk", bufs=3) as pbk:
-        warm = const.tile([P, 1], F32)
-        nc.vector.memset(warm[:], 0.0)
-        warm2 = const.tile([P, 1], F32)
-        nc.scalar.activation(out=warm2[:], in_=warm[:], func=ACT.Exp)
+    ) as xin, tc.tile_pool(name="state", bufs=CHUNKS // 2) as state, tc.tile_pool(
+        name="quant", bufs=2
+    ) as quant, tc.tile_pool(name="work", bufs=2) as work, tc.tile_pool(
+        name="outs", bufs=3
+    ) as outs, tc.psum_pool(name="front", bufs=3) as front, tc.psum_pool(
+        name="gate", bufs=1
+    ) as gate, tc.psum_pool(name="rows", bufs=3) as rows, tc.manual_schedule():
+        kept = {}
 
-        ident = const.tile([P, P], F32)
-        make_identity(nc, ident[:])
+        def absent(c):
+            return c < 0 or c >= CHUNKS
+
+        def by_tile(ap):
+            return ap.rearrange("p (t h) -> p t h", h=H)
+
+        def new(pool, name, c):
+            kept[(name, c)] = pool.tile([P, CW], F32, tag=name, name=name)
+            return kept[(name, c)]
+
+        def load_x(c, nm):
+            if absent(c):
+                return
+            x_sb = xin.tile([P, TPC * K], BF16, tag="x" + nm, name="x" + nm)
+            nc.sync.dma_start(
+                out=x_sb[:].rearrange("p (t k) -> p t k", t=TPC),
+                in_=x_views[nm][:, c * TPC : (c + 1) * TPC, :],
+            )
+            kept[("x" + nm, c)] = x_sb
+
+        def load_state(c):
+            if absent(c) or c % 2 == 1:
+                return
+            for nm in ("m", "n", "c"):
+                st = state.tile([P, 2 * CW], BF16, tag="st" + nm, name="st" + nm)
+                nc.sync.dma_start(out=by_tile(st[:]), in_=state_views[nm][:, c * TPC : (c + 2) * TPC, :])
+                kept[(nm + "_prev", c)] = st[:, 0:CW]
+                kept[(nm + "_prev", c + 1)] = st[:, CW : 2 * CW]
+
+        def store(c, nm):
+            if absent(c):
+                return
+            nc.sync.dma_start(
+                out=out_views[nm][:, c * TPC : (c + 1) * TPC, :], in_=by_tile(kept[(nm + "_t", c)][:])
+            )
+
+        load_x(0, "c")
+        bias_rows = const.tile([P, P], BF16)
+        nc.vector.memset(bias_rows[:], 0.0)
+        for g in range(GATES):
+            nc.sync.dma_start(out=bias_rows[g : g + 1, :], in_=biases[g].unsqueeze(0))
+        w_raw = const.tile([P, GATES, 4, H], BF16)
+        for g in range(GATES):
+            nc.sync.dma_start(
+                out=w_raw[:, g, :, :].rearrange("p (u e) c -> p u e c", u=2),
+                in_=weights[g].rearrange("(u q e) c -> q u e c", u=2, e=2),
+            )
+        load_x(0, "l")
+        load_state(0)
+        for c in (1, 2):
+            load_x(c, "c")
+            load_x(c, "l")
+
+        zero = const.tile([P, 1], F32)
+        nc.vector.memset(zero[:], 0.0)
+        one = const.tile([P, 1], F32)
+        nc.scalar.activation(out=one[:], in_=zero[:], func=ACT.Exp)
         half = const.tile([P, TPC], F32)
         nc.vector.memset(half[:], 0.5)
+        ident = const.tile([P, P], F32)
+        make_identity(nc, ident[:])
+        ident_bf = const.tile([P, P], BF16)
+        nc.vector.tensor_copy(out=ident_bf[:], in_=ident[:])
 
-        w_list = [wi_w, wf_w, wk_w[0], wq_w[0], wv_w[0], wo_w]
-        b_list = [wi_b, wf_b, wk_b, wv_b, wq_b, wo_b]
-        wraw = const.tile([P, 6, 4, H], BF16)
-        braw = const.tile([P, P], BF16)
-        nc.vector.memset(braw[:], 0.0)
-        wgrp = const.tile([P, 6, H, 4], BF16, align_bytes=64)
-        wcodes = const.tile([P, 6 * H], U32, align_bytes=64)
-        wscales = const.tile([P, 6 * H], U8, align_bytes=64)
-        bf32 = const.tile([P, P], F32)
-        bias = const.tile([P, 8], F32)
-        bks = const.tile([P, 1], F32)
-        boh = const.tile([P, 1], F32)
-
-        def load_bias(r):
-            nc.sync.dma_start(out=braw[r : r + 1, :], in_=b_list[r].unsqueeze(0))
-
-        def load_weight(g):
-            nc.sync.dma_start(
-                out=wraw[:, g, :, :].rearrange("p (u e) c -> p u e c", u=2),
-                in_=w_list[g].rearrange("(u q e) c -> q u e c", u=2, e=2),
-            )
-
-        def quantise_weights(g0, g1):
-            nc.vector.tensor_copy(
-                out=wgrp[:, g0:g1], in_=wraw[:, g0:g1].rearrange("p g t c -> p g c t")
-            )
-            nc.vector.quantize_mx(
-                out=wcodes[:, g0 * H : g1 * H].bitcast(FP8X4),
-                scales=wscales[:, g0 * H : g1 * H],
-                in_=wgrp[:, g0:g1].rearrange("p g c t -> p (g c t)"),
-            )
-
-        def spread_biases():
-            nc.vector.tensor_copy(out=bf32[:], in_=braw[:])
-            bps = pbk.tile([P, CW], F32, tag="bk", name="bps")
-            nc.tensor.transpose(bps[:, 0:P], bf32[:], ident[:])
-            nc.vector.tensor_copy(out=bias[:, 0:6], in_=bps[:, 0:6])
-            nc.vector.tensor_scalar_mul(out=bks[:], in0=bias[:, 2:3], scalar1=k_scale)
-            nc.vector.tensor_scalar_mul(out=boh[:], in0=bias[:, 5:6], scalar1=0.5)
-
-        st_tiles = {}
-
-        def load_x(x_view, c, nm):
-            xt_sb = xin.tile([P, TPC * K], BF16, tag="x" + nm, name="x" + nm)
-            nc.sync.dma_start(
-                out=xt_sb[:].rearrange("p (t k) -> p t k", t=TPC),
-                in_=x_view[:, c * TPC : (c + 1) * TPC, :],
-            )
-            return xt_sb
-
-        def quantise_x(xt_sb, nm):
-            xw = xt_sb[:].bitcast(F32)
-            grouped = grp.tile([P, 4 * CW], BF16, tag="g" + nm, name="g" + nm, align_bytes=64)
-            g32 = grouped[:].bitcast(F32)
-            for bnk in range(2):
-                xt = pxt.tile([P, CW], F32, tag="xt", name="xt")
-                for tt in range(2):
-                    t = 2 * bnk + tt
-                    for u in range(2):
-                        nc.tensor.transpose(
-                            xt[:, u * 256 + tt * P : u * 256 + (tt + 1) * P],
-                            xw[:, t * 256 + u * P : t * 256 + (u + 1) * P],
-                            ident[:],
-                        )
-                nc.scalar.copy(
-                    out=g32[:, bnk * CW : (bnk + 1) * CW].rearrange("p (b u) -> p b u", u=2),
-                    in_=xt[:].rearrange("p (u b) -> p b u", u=2),
-                )
-            codes = grp.tile([P, CW], U32, tag="c" + nm, name="c" + nm, align_bytes=64)
-            scales = grp.tile([P, CW], U8, tag="s" + nm, name="s" + nm, align_bytes=64)
-            nc.vector.quantize_mx(out=codes[:].bitcast(FP8X4), scales=scales[:], in_=grouped[:])
-            return codes, scales
-
-        def project(g, xq):
-            acc = pmx.tile([P, CW], F32, tag="mx", name="acc")
-            nc.tensor.matmul_mx(
-                out=acc[:],
-                lhsT=wcodes[:, g * H : (g + 1) * H].bitcast(FP8X4),
-                lhsT_scale=wscales[:, g * H : (g + 1) * H],
-                rhs=xq[0][:].bitcast(FP8X4),
-                rhs_scale=xq[1][:],
+        bias_f32 = const.tile([P, P], F32)
+        nc.vector.tensor_copy(out=bias_f32[:], in_=bias_rows[:])
+        spread = rows.tile([P, CW], F32, tag="rows", name="spread")
+        nc.tensor.transpose(spread[:, 0:P], bias_f32[:], ident[:])
+        for g in (G_I, G_F):
+            nc.tensor.matmul(
+                out=spread[:, (g + 1) * P : (g + 2) * P],
+                lhsT=ident_bf[:, g : g + 1].to_broadcast([P, P]),
+                rhs=bias_rows[:],
                 start=True,
                 stop=True,
             )
-            return acc
 
-        def back(src, nm):
-            dst = pbk.tile([P, CW], F32, tag="bk", name="bk" + nm)
-            if nm in ("tp", "k", "q"):
-                for rep in range(2):
-                    nc.tensor.matmul_mx(
-                        out=dst[:],
-                        lhsT=wcodes[:, 0:H].bitcast(FP8X4),
-                        lhsT_scale=wscales[:, 0:H],
-                        rhs=wcodes[:, 0:CW].bitcast(FP8X4),
-                        rhs_scale=wscales[:, 0:CW],
-                        start=True,
-                        stop=True,
+        w_grouped = const.tile([P, GATES, H, 4], BF16, align_bytes=64)
+        w_codes = const.tile([P, GATES * H], U32, align_bytes=64)
+        w_scales = const.tile([P, GATES * H], U8, align_bytes=64)
+
+        def quantise_weights(g0, g1):
+            nc.vector.tensor_copy(
+                out=w_grouped[:, g0:g1], in_=w_raw[:, g0:g1].rearrange("p g t c -> p g c t")
+            )
+            nc.vector.quantize_mx(
+                out=w_codes[:, g0 * H : g1 * H].bitcast(FP8X4),
+                scales=w_scales[:, g0 * H : g1 * H],
+                in_=w_grouped[:, g0:g1].rearrange("p g c t -> p (g c t)"),
+            )
+
+        quantise_weights(G_I, G_F + 1)
+        bias_col = const.tile([P, GATES], F32)
+        nc.vector.tensor_copy(out=bias_col[:], in_=spread[:, 0:GATES])
+        bk_scaled = const.tile([P, 1], F32)
+        nc.vector.tensor_scalar_mul(out=bk_scaled[:], in0=bias_col[:, G_K : G_K + 1], scalar1=k_scale)
+        bo_half = const.tile([P, 1], F32)
+        nc.vector.tensor_scalar_mul(out=bo_half[:], in0=bias_col[:, G_O : G_O + 1], scalar1=0.5)
+        bi_row = const.tile([P, H], F32)
+        nc.vector.tensor_copy(out=bi_row[:], in_=spread[:, (G_I + 1) * P : (G_I + 2) * P])
+        bf_minus_bi_row = const.tile([P, H], F32)
+        nc.vector.tensor_tensor(
+            out=bf_minus_bi_row[:], in0=spread[:, (G_F + 1) * P : (G_F + 2) * P], in1=bi_row[:], op=ALU.subtract
+        )
+        quantise_weights(G_K, G_Q + 1)
+        quantise_weights(G_V, G_O + 1)
+
+        def over_tiles(row):
+            return row[:].unsqueeze(1).to_broadcast([P, TPC, H])
+
+        def transpose_x(c, nm, half_no):
+            if absent(c):
+                return
+            words = kept[("x" + nm, c)][:].bitcast(F32)
+            bank = front.tile([P, CW], F32, tag="front", name="xT")
+            for tt in range(2):
+                t = 2 * half_no + tt
+                for u in range(2):
+                    nc.tensor.transpose(
+                        bank[:, u * 256 + tt * P : u * 256 + (tt + 1) * P],
+                        words[:, t * 256 + u * P : t * 256 + (u + 1) * P],
+                        ident[:],
                     )
+            kept[("xT" + nm, c, half_no)] = bank
+
+        def regroup_x(c, nm, half_no):
+            if absent(c):
+                return
+            if half_no == 0:
+                kept[("grouped" + nm, c)] = quant.tile(
+                    [P, 4 * CW], BF16, tag="grouped" + nm, name="grouped" + nm, align_bytes=64
+                )
+            words = kept[("grouped" + nm, c)][:].bitcast(F32)
+            nc.scalar.copy(
+                out=words[:, half_no * CW : (half_no + 1) * CW].rearrange("p (b u) -> p b u", u=2),
+                in_=kept[("xT" + nm, c, half_no)][:].rearrange("p (u b) -> p b u", u=2),
+            )
+
+        def quantise_x(c, nm):
+            if absent(c):
+                return
+            codes = quant.tile([P, CW], U32, tag="codes" + nm, name="codes" + nm, align_bytes=64)
+            scales = quant.tile([P, CW], U8, tag="scales" + nm, name="scales" + nm, align_bytes=64)
+            nc.vector.quantize_mx(
+                out=codes[:].bitcast(FP8X4), scales=scales[:], in_=kept[("grouped" + nm, c)][:]
+            )
+            kept[("mx" + nm, c)] = (codes, scales)
+
+        def project_rows(c, g, nm, name):
+            if absent(c):
+                return
+            codes, scales = kept[("mx" + nm, c)]
+            acc = gate.tile([P, CW], F32, tag=name, name=name)
             for t in range(TPC):
-                nc.tensor.transpose(dst[:, t * H : (t + 1) * H], src[:, t * P : (t + 1) * P], ident[:])
-            return dst
+                nc.tensor.matmul_mx(
+                    out=acc[:, t * H : (t + 1) * H],
+                    lhsT=codes[:, t * P : (t + 1) * P].bitcast(FP8X4),
+                    lhsT_scale=scales[:, t * P : (t + 1) * P],
+                    rhs=w_codes[:, g * H : (g + 1) * H].bitcast(FP8X4),
+                    rhs_scale=w_scales[:, g * H : (g + 1) * H],
+                    start=True,
+                    stop=True,
+                )
+            kept[(name, c)] = acc
 
-        for r in range(3):
-            load_bias(r)
-        x_first = [load_x(xc_v, 0, "c")]
-        for r in range(3, 6):
-            load_bias(r)
-        for g in range(4):
-            load_weight(g)
-        x_first.append(load_x(xl_v, 0, "l"))
-        for g in range(4, 6):
-            load_weight(g)
+        def project_cols(c, g, nm, name, func, bias_ap, scale):
+            if absent(c):
+                return
+            codes, scales = kept[("mx" + nm, c)]
+            acc = front.tile([P, CW], F32, tag="front", name="acc")
+            nc.tensor.matmul_mx(
+                out=acc[:],
+                lhsT=w_codes[:, g * H : (g + 1) * H].bitcast(FP8X4),
+                lhsT_scale=w_scales[:, g * H : (g + 1) * H],
+                rhs=codes[:].bitcast(FP8X4),
+                rhs_scale=scales[:],
+                start=True,
+                stop=True,
+            )
+            kept[("acc" + name, c)] = (acc, func, bias_ap, scale)
 
-        for c in range(NCH):
-            if c % 2 == 0:
-                for nm, view in (("m", m_v), ("n", n_v), ("c", c_v)):
-                    st = state.tile([P, 2 * CW], BF16, tag="st" + nm, name="st" + nm)
-                    nc.sync.dma_start(
-                        out=st[:].rearrange("p (t h) -> p t h", h=H),
-                        in_=view[:, c * TPC : (c + 2) * TPC, :],
-                    )
-                    st_tiles[nm] = st
-            lo = (c % 2) * CW
-            m_in = st_tiles["m"][:, lo : lo + CW]
-            n_in = st_tiles["n"][:, lo : lo + CW]
-            c_in = st_tiles["c"][:, lo : lo + CW]
+        def leave_psum(c, name):
+            if absent(c):
+                return
+            acc, func, bias_ap, scale = kept[("acc" + name, c)]
+            nc.scalar.activation(
+                out=new(work, name + "_cols", c)[:], in_=acc[:], func=func, bias=bias_ap, scale=scale
+            )
 
-            if c == 0:
-                xcq = quantise_x(x_first[0], "c")
-                spread_biases()
-                quantise_weights(0, 2)
-                quantise_weights(2, 4)
-                xlq = quantise_x(x_first[1], "l")
-                quantise_weights(4, 6)
-            else:
-                xcq = quantise_x(load_x(xc_v, c, "c"), "c")
-                xlq = quantise_x(load_x(xl_v, c, "l"), "l")
+        def to_rows(c, name):
+            if absent(c):
+                return
+            src = kept[(name + "_cols", c)]
+            bank = rows.tile([P, CW], F32, tag="rows", name=name + "_rows")
+            for t in range(TPC):
+                nc.tensor.transpose(bank[:, t * H : (t + 1) * H], src[:, t * P : (t + 1) * P], ident[:])
+            kept[(name, c)] = bank
 
-            acc_i = project(0, xcq)
-            it_b = bl.tile([P, CW], F32, tag="it", name="it_b")
-            nc.scalar.activation(out=it_b[:], in_=acc_i[:], func=ACT.Identity, bias=bias[:, 0:1], scale=1.0)
-            acc_f = project(1, xcq)
-            tp_b = bl.tile([P, CW], F32, tag="tp", name="tp_b")
-            nc.vector.scalar_tensor_tensor(
-                out=tp_b[:], in0=acc_f[:], scalar=bias[:, 1:2], in1=it_b[:], op0=ALU.add, op1=ALU.subtract
-            )
-            acc_k = project(2, xcq)
-            k_b = bl.tile([P, CW], F32, tag="k", name="k_b")
-            nc.scalar.activation(out=k_b[:], in_=acc_k[:], func=ACT.Identity, bias=bks[:], scale=k_scale)
-            acc_v = project(4, xlq)
-            v_b = bl.tile([P, CW], F32, tag="v", name="v_b")
-            nc.scalar.activation(out=v_b[:], in_=acc_v[:], func=ACT.Identity, bias=bias[:, 3:4], scale=1.0)
-            acc_q = project(3, xcq)
-            q_b = bl.tile([P, CW], F32, tag="q", name="q_b")
-            nc.scalar.activation(out=q_b[:], in_=acc_q[:], func=ACT.Identity, bias=bias[:, 4:5], scale=1.0)
-            acc_o = project(5, xlq)
-            th_b = bl.tile([P, CW], F32, tag="th", name="th_b")
-            nc.scalar.activation(out=th_b[:], in_=acc_o[:], func=ACT.Tanh, bias=boh[:], scale=0.5)
+        def tensor_tensor(engine, pool, out_name, c, a, b, op):
+            if absent(c):
+                return
+            engine.tensor_tensor(out=new(pool, out_name, c)[:], in0=kept[(a, c)][:], in1=kept[(b, c)][:], op=op)
 
-            tp_a = back(tp_b, "tp")
-            d = al.tile([P, CW], F32, tag="d", name="d")
-            nc.vector.tensor_tensor(out=d[:], in0=tp_a[:], in1=m_in, op=ALU.add)
-            e1 = al.tile([P, CW], F32, tag="e1", name="e1")
-            nc.scalar.activation(out=e1[:], in_=d[:], func=ACT.Exp, scale=-1.0)
-            e2 = al.tile([P, CW], F32, tag="e2", name="e2")
-            nc.scalar.activation(out=e2[:], in_=d[:], func=ACT.Exp, scale=1.0)
-            it_a = back(it_b, "it")
-            m_o = outp.tile([P, CW], F32, tag="mo", name="m_o")
+        def scalar_then_tensor(pool, out_name, c, a, scalar, op0, b, op1):
+            if absent(c):
+                return
             nc.vector.scalar_tensor_tensor(
-                out=m_o[:], in0=d[:], scalar=0.0, in1=it_a[:], op0=ALU.max, op1=ALU.add
+                out=new(pool, out_name, c)[:],
+                in0=kept[(a, c)][:],
+                scalar=scalar,
+                in1=kept[(b, c)][:],
+                op0=op0,
+                op1=op1,
             )
-            nc.sync.dma_start(
-                out=m_ov[:, c * TPC : (c + 1) * TPC, :], in_=m_o[:].rearrange("p (t h) -> p t h", h=H)
+
+        def add_row(pool, out_name, c, a, row):
+            if absent(c):
+                return
+            nc.gpsimd.tensor_tensor(
+                out=by_tile(new(pool, out_name, c)[:]), in0=by_tile(kept[(a, c)][:]), in1=over_tiles(row), op=ALU.add
             )
-            k_a = back(k_b, "k")
-            ik = al.tile([P, CW], F32, tag="ik", name="ik")
-            nc.vector.scalar_tensor_tensor(
-                out=ik[:], in0=e1[:], scalar=1.0, in1=k_a[:], op0=ALU.min, op1=ALU.mult
-            )
-            v_a = back(v_b, "v")
-            ikv = al.tile([P, CW], F32, tag="ikv", name="ikv")
-            nc.vector.tensor_tensor(out=ikv[:], in0=v_a[:], in1=ik[:], op=ALU.mult)
-            fn = al.tile([P, CW], F32, tag="fn", name="fn")
-            nc.vector.scalar_tensor_tensor(
-                out=fn[:], in0=e2[:], scalar=1.0, in1=n_in, op0=ALU.min, op1=ALU.mult
-            )
-            fc = al.tile([P, CW], F32, tag="fc", name="fc")
-            nc.vector.scalar_tensor_tensor(
-                out=fc[:], in0=e2[:], scalar=1.0, in1=c_in, op0=ALU.min, op1=ALU.mult
-            )
-            n_o = outp.tile([P, CW], F32, tag="no", name="n_o")
-            nc.vector.tensor_tensor(out=n_o[:], in0=fn[:], in1=ik[:], op=ALU.add)
-            nc.sync.dma_start(
-                out=n_ov[:, c * TPC : (c + 1) * TPC, :], in_=n_o[:].rearrange("p (t h) -> p t h", h=H)
-            )
-            c_o = outp.tile([P, CW], F32, tag="co", name="c_o")
-            nc.vector.tensor_tensor(out=c_o[:], in0=fc[:], in1=ikv[:], op=ALU.add)
-            nc.sync.dma_start(
-                out=c_ov[:, c * TPC : (c + 1) * TPC, :], in_=c_o[:].rearrange("p (t h) -> p t h", h=H)
-            )
-            q_a = back(q_b, "q")
-            nq = al.tile([P, CW], F32, tag="nq", name="nq")
-            nc.vector.tensor_tensor(out=nq[:], in0=q_a[:], in1=n_o[:], op=ALU.mult)
-            cq = al.tile([P, CW], F32, tag="cq", name="cq")
-            nc.vector.tensor_tensor(out=cq[:], in0=q_a[:], in1=c_o[:], op=ALU.mult)
-            sq = al.tile([P, CW], F32, tag="sq", name="sq")
-            ss = small.tile([P, TPC], F32, tag="ss", name="ss")
+
+        def exponential(c, out_name, sign):
+            if absent(c):
+                return
+            nc.scalar.activation(out=new(work, out_name, c)[:], in_=kept[("d", c)][:], func=ACT.Exp, scale=sign)
+
+        def sum_of_squares(c):
+            if absent(c):
+                return
+            squares = work.tile([P, CW], F32, tag="squares", name="squares")
+            ss = work.tile([P, TPC], F32, tag="ss", name="ss")
             for t in range(TPC):
                 nc.scalar.activation(
-                    out=sq[:, t * H : (t + 1) * H],
-                    in_=nq[:, t * H : (t + 1) * H],
+                    out=squares[:, t * H : (t + 1) * H],
+                    in_=kept[("nq", c)][:, t * H : (t + 1) * H],
                     func=ACT.Square,
                     scale=2.0,
                     accum_out=ss[:, t : t + 1],
                 )
-            th_a = back(th_b, "th")
-            h1 = al.tile([P, CW], F32, tag="h1", name="h1")
-            nc.vector.scalar_tensor_tensor(
-                out=h1[:], in0=th_a[:], scalar=1.0, in1=cq[:], op0=ALU.add, op1=ALU.mult
-            )
-            den = small.tile([P, TPC], F32, tag="den", name="den")
-            nc.gpsimd.tensor_tensor(out=den[:], in0=ss[:], in1=half[:], op=ALU.pow)
-            den2 = small.tile([P, TPC], F32, tag="den2", name="den2")
-            nc.vector.tensor_scalar_add(out=den2[:], in0=den[:], scalar1=2.0e-6)
-            rden = small.tile([P, TPC], F32, tag="rden", name="rden")
-            nc.vector.reciprocal(out=rden[:], in_=den2[:])
-            h_o = outp.tile([P, CW], F32, tag="ho", name="h_o")
+            kept[("ss", c)] = ss
+
+        def small(c, name):
+            kept[(name, c)] = work.tile([P, TPC], F32, tag=name, name=name)
+            return kept[(name, c)]
+
+        def square_root(c):
+            if absent(c):
+                return
+            nc.gpsimd.tensor_tensor(out=small(c, "root")[:], in0=kept[("ss", c)][:], in1=half[:], op=ALU.pow)
+
+        def add_epsilon(c):
+            if absent(c):
+                return
+            nc.vector.tensor_scalar_add(out=small(c, "denom2")[:], in0=kept[("root", c)][:], scalar1=2.0e-6)
+
+        def reciprocal(c):
+            if absent(c):
+                return
+            nc.vector.reciprocal(out=small(c, "scale")[:], in_=kept[("denom2", c)][:])
+
+        def scale_rows(c):
+            if absent(c):
+                return
+            h_t = new(outs, "h_t", c)
             for t in range(TPC):
-                nc.gpsimd.tensor_scalar(
-                    out=h_o[:, t * H : (t + 1) * H],
-                    in0=h1[:, t * H : (t + 1) * H],
-                    scalar1=rden[:, t : t + 1],
-                    scalar2=0.0,
-                    op0=ALU.mult,
-                    op1=ALU.add,
+                nc.vector.tensor_scalar_mul(
+                    out=h_t[:, t * H : (t + 1) * H],
+                    in0=kept[("h_unscaled", c)][:, t * H : (t + 1) * H],
+                    scalar1=kept[("scale", c)][:, t : t + 1],
                 )
-            nc.sync.dma_start(
-                out=h_ov[:, c * TPC : (c + 1) * TPC, :], in_=h_o[:].rearrange("p (t h) -> p t h", h=H)
-            )
+
+        for j in range(-2, CHUNKS + 2):
+            ahead, gates, cell, last, done = j + 2, j + 1, j, j - 1, j - 2
+
+            tensor_tensor(nc.vector, work, "u", gates, "f_sum", "m_shifted", ALU.add)
+            scalar_then_tensor(work, "ik", cell, "exp_minus_d", 1.0, ALU.min, "k", ALU.mult)
+            tensor_tensor(nc.vector, work, "d", gates, "u", "i_sum", ALU.subtract)
+            scalar_then_tensor(work, "fn", cell, "exp_d", 1.0, ALU.min, "n_prev", ALU.mult)
+            tensor_tensor(nc.vector, work, "nq", last, "q", "n_t", ALU.mult)
+            leave_psum(gates, "k")
+            to_rows(cell, "v")
+            add_row(work, "m_shifted", ahead, "m_prev", bf_minus_bi_row)
+            tensor_tensor(nc.gpsimd, outs, "n_t", cell, "fn", "ik", ALU.add)
+
+            for nm in ("c", "l"):
+                for half_no in range(2):
+                    transpose_x(ahead, nm, half_no)
+                    regroup_x(ahead, nm, half_no)
+            load_x(j + 5, "c")
+            load_x(j + 5, "l")
+            load_state(j + 4)
+            store(cell, "n")
+
+            tensor_tensor(nc.vector, work, "ikv", cell, "v", "ik", ALU.mult)
+            scalar_then_tensor(work, "m_less_bi", gates, "d", 0.0, ALU.max, "i_sum", ALU.add)
+            scalar_then_tensor(work, "fc", cell, "exp_d", 1.0, ALU.min, "c_prev", ALU.mult)
+            tensor_tensor(nc.vector, work, "cq", last, "q", "c_t", ALU.mult)
+            add_row(outs, "m_t", gates, "m_less_bi", bi_row)
+            tensor_tensor(nc.gpsimd, outs, "c_t", cell, "fc", "ikv", ALU.add)
+
+            to_rows(last, "o")
+            project_cols(gates, G_V, "l", "v", ACT.Identity, bias_col[:, G_V : G_V + 1], 1.0)
+            leave_psum(gates, "v")
+            project_cols(gates, G_O, "l", "o", ACT.Tanh, bo_half[:], 0.5)
+            leave_psum(gates, "o")
+            project_cols(gates, G_Q, "c", "q", ACT.Identity, bias_col[:, G_Q : G_Q + 1], 1.0)
+            leave_psum(gates, "q")
+            to_rows(gates, "k")
+
+            quantise_x(ahead, "c")
+            add_epsilon(done)
+            scalar_then_tensor(work, "h_unscaled", last, "o", 1.0, ALU.add, "cq", ALU.mult)
+            reciprocal(done)
+            quantise_x(ahead, "l")
+            scale_rows(done)
+            sum_of_squares(last)
+            exponential(gates, "exp_minus_d", -1.0)
+            exponential(gates, "exp_d", 1.0)
+            square_root(last)
+            store(gates, "m")
+            store(cell, "c")
+            store(done, "h")
+
+            project_rows(ahead, G_F, "c", "f_sum")
+            project_rows(ahead, G_I, "c", "i_sum")
+            project_cols(ahead, G_K, "c", "k", ACT.Identity, bk_scaled[:], k_scale)
+            to_rows(cell, "q")

@@ -109,11 +109,19 @@ def tile_mlstmblock_pb_t_kernel(
         def load_state(c):
             if absent(c) or c % 2 == 1:
                 return
-            for nm in ("m", "n", "c"):
+            for nm in ("n", "c"):
                 st = state.tile([P, 2 * CW], BF16, tag="st" + nm, name="st" + nm)
                 nc.sync.dma_start(out=by_tile(st[:]), in_=state_views[nm][:, c * TPC : (c + 2) * TPC, :])
                 kept[(nm + "_prev", c)] = st[:, 0:CW]
                 kept[(nm + "_prev", c + 1)] = st[:, CW : 2 * CW]
+
+        m_all = const.tile([P, CHUNKS * CW], BF16)
+
+        def load_m(first, count):
+            nc.sync.dma_start(
+                out=by_tile(m_all[:, first * CW : (first + count) * CW]),
+                in_=state_views["m"][:, first * TPC : (first + count) * TPC, :],
+            )
 
         def store(c, nm):
             if absent(c):
@@ -134,10 +142,13 @@ def tile_mlstmblock_pb_t_kernel(
                 in_=weights[g].rearrange("(u q e) c -> q u e c", u=2, e=2),
             )
         load_x(0, "l")
+        load_m(0, CHUNKS // 2)
         load_state(0)
-        for c in (1, 2):
-            load_x(c, "c")
-            load_x(c, "l")
+        load_x(1, "c")
+        load_x(1, "l")
+        load_m(CHUNKS // 2, CHUNKS // 2)
+        load_x(2, "c")
+        load_x(2, "l")
 
         zero = const.tile([P, 1], F32)
         nc.vector.memset(zero[:], 0.0)
@@ -195,6 +206,16 @@ def tile_mlstmblock_pb_t_kernel(
 
         def over_tiles(row):
             return row[:].unsqueeze(1).to_broadcast([P, TPC, H])
+
+        m_shifted = const.tile([P, CHUNKS * CW], F32)
+        for c in range(CHUNKS):
+            nc.gpsimd.tensor_tensor(
+                out=by_tile(m_shifted[:, c * CW : (c + 1) * CW]),
+                in0=by_tile(m_all[:, c * CW : (c + 1) * CW]),
+                in1=over_tiles(bf_minus_bi_row),
+                op=ALU.add,
+            )
+            kept[("m_shifted", c)] = m_shifted[:, c * CW : (c + 1) * CW]
 
         def transpose_x(c, nm, half_no):
             if absent(c):
@@ -368,7 +389,6 @@ def tile_mlstmblock_pb_t_kernel(
             tensor_tensor(nc.vector, work, "nq", last, "q", "n_t", ALU.mult)
             leave_psum(gates, "k")
             to_rows(cell, "v")
-            add_row(work, "m_shifted", ahead, "m_prev", bf_minus_bi_row)
             tensor_tensor(nc.gpsimd, outs, "n_t", cell, "fn", "ik", ALU.add)
 
             for nm in ("c", "l"):

@@ -109,11 +109,14 @@ def tile_mlstmblock_pb_t_kernel(
         def load_state(c):
             if absent(c) or c % 2 == 1:
                 return
-            for nm in ("n", "c"):
-                st = state.tile([P, 2 * CW], BF16, tag="st" + nm, name="st" + nm)
-                nc.sync.dma_start(out=by_tile(st[:]), in_=state_views[nm][:, c * TPC : (c + 2) * TPC, :])
-                kept[(nm + "_prev", c)] = st[:, 0:CW]
-                kept[(nm + "_prev", c + 1)] = st[:, CW : 2 * CW]
+            st = state.tile([P, 2, 2, CW], BF16, tag="nc_prev", name="nc_prev")
+            for s, nm in enumerate(("n", "c")):
+                nc.sync.dma_start(
+                    out=st[:, :, s, :],
+                    in_=state_views[nm][:, c * TPC : (c + 2) * TPC, :].rearrange("p (a t) h -> p a (t h)", a=2),
+                )
+            kept[("nc_prev", c)] = st[:, 0, :, :]
+            kept[("nc_prev", c + 1)] = st[:, 1, :, :]
 
         m_all = const.tile([P, CHUNKS * CW], BF16)
 
@@ -235,25 +238,23 @@ def tile_mlstmblock_pb_t_kernel(
         def regroup_x(c, nm, half_no):
             if absent(c):
                 return
-            if half_no == 0:
-                kept[("grouped" + nm, c)] = quant.tile(
-                    [P, 4 * CW], BF16, tag="grouped" + nm, name="grouped" + nm, align_bytes=64
-                )
-            words = kept[("grouped" + nm, c)][:].bitcast(F32)
+            if ("grouped", c) not in kept:
+                kept[("grouped", c)] = quant.tile([P, 2 * 4 * CW], BF16, tag="grouped", name="grouped", align_bytes=64)
+            words = kept[("grouped", c)][:].bitcast(F32)
+            part = 2 * ("c", "l").index(nm) + half_no
             nc.scalar.copy(
-                out=words[:, half_no * CW : (half_no + 1) * CW].rearrange("p (b u) -> p b u", u=2),
+                out=words[:, part * CW : (part + 1) * CW].rearrange("p (b u) -> p b u", u=2),
                 in_=kept[("xT" + nm, c, half_no)][:].rearrange("p (u b) -> p b u", u=2),
             )
 
-        def quantise_x(c, nm):
+        def quantise_x(c):
             if absent(c):
                 return
-            codes = quant.tile([P, CW], U32, tag="codes" + nm, name="codes" + nm, align_bytes=64)
-            scales = quant.tile([P, CW], U8, tag="scales" + nm, name="scales" + nm, align_bytes=64)
-            nc.vector.quantize_mx(
-                out=codes[:].bitcast(FP8X4), scales=scales[:], in_=kept[("grouped" + nm, c)][:]
-            )
-            kept[("mx" + nm, c)] = (codes, scales)
+            codes = quant.tile([P, 2 * CW], U32, tag="codes", name="codes", align_bytes=64)
+            scales = quant.tile([P, 2 * CW], U8, tag="scales", name="scales", align_bytes=64)
+            nc.vector.quantize_mx(out=codes[:].bitcast(FP8X4), scales=scales[:], in_=kept[("grouped", c)][:])
+            kept[("mxc", c)] = (codes[:, 0:CW], scales[:, 0:CW])
+            kept[("mxl", c)] = (codes[:, CW : 2 * CW], scales[:, CW : 2 * CW])
 
         def project_rows(c, g, nm, name):
             if absent(c):
@@ -329,6 +330,21 @@ def tile_mlstmblock_pb_t_kernel(
                 out=by_tile(new(pool, out_name, c)[:]), in0=by_tile(kept[(a, c)][:]), in1=over_tiles(row), op=ALU.add
             )
 
+        def forget_states(c):
+            if absent(c):
+                return
+            both = work.tile([P, 2 * CW], F32, tag="f_states", name="f_states")
+            nc.vector.scalar_tensor_tensor(
+                out=both[:].rearrange("p (s w) -> p s w", s=2),
+                in0=kept[("exp_d", c)][:].unsqueeze(1).to_broadcast([P, 2, CW]),
+                scalar=1.0,
+                in1=kept[("nc_prev", c)],
+                op0=ALU.min,
+                op1=ALU.mult,
+            )
+            kept[("fn", c)] = both[:, 0:CW]
+            kept[("fc", c)] = both[:, CW : 2 * CW]
+
         def exponential(c, out_name, sign):
             if absent(c):
                 return
@@ -371,21 +387,21 @@ def tile_mlstmblock_pb_t_kernel(
         def scale_rows(c):
             if absent(c):
                 return
-            h_t = new(outs, "h_t", c)
-            for t in range(TPC):
-                nc.vector.tensor_scalar_mul(
-                    out=h_t[:, t * H : (t + 1) * H],
-                    in0=kept[("h_unscaled", c)][:, t * H : (t + 1) * H],
-                    scalar1=kept[("scale", c)][:, t : t + 1],
-                )
+            nc.vector.tensor_tensor(
+                out=by_tile(new(outs, "h_t", c)[:]),
+                in0=by_tile(kept[("h_unscaled", c)][:]),
+                in1=kept[("scale", c)][:].unsqueeze(2).to_broadcast([P, TPC, H]),
+                op=ALU.mult,
+            )
 
-        for j in range(-2, CHUNKS + 2):
-            ahead, gates, cell, last, done = j + 2, j + 1, j, j - 1, j - 2
+        for j in range(-3, CHUNKS + 2):
+            far, ahead, gates, cell, last, done = j + 3, j + 2, j + 1, j, j - 1, j - 2
 
+            quantise_x(ahead)
             tensor_tensor(nc.vector, work, "u", gates, "f_sum", "m_shifted", ALU.add)
             scalar_then_tensor(work, "ik", cell, "exp_minus_d", 1.0, ALU.min, "k", ALU.mult)
             tensor_tensor(nc.vector, work, "d", gates, "u", "i_sum", ALU.subtract)
-            scalar_then_tensor(work, "fn", cell, "exp_d", 1.0, ALU.min, "n_prev", ALU.mult)
+            forget_states(cell)
             tensor_tensor(nc.vector, work, "nq", last, "q", "n_t", ALU.mult)
             leave_psum(gates, "k")
             to_rows(cell, "v")
@@ -393,21 +409,24 @@ def tile_mlstmblock_pb_t_kernel(
 
             for nm in ("c", "l"):
                 for half_no in range(2):
-                    transpose_x(ahead, nm, half_no)
-                    regroup_x(ahead, nm, half_no)
-            load_x(j + 5, "c")
-            load_x(j + 5, "l")
+                    transpose_x(far, nm, half_no)
+                    regroup_x(far, nm, half_no)
+            to_rows(last, "o")
+            load_x(j + 6, "c")
+            load_x(j + 6, "l")
             load_state(j + 4)
             store(cell, "n")
 
             tensor_tensor(nc.vector, work, "ikv", cell, "v", "ik", ALU.mult)
-            scalar_then_tensor(work, "m_less_bi", gates, "d", 0.0, ALU.max, "i_sum", ALU.add)
-            scalar_then_tensor(work, "fc", cell, "exp_d", 1.0, ALU.min, "c_prev", ALU.mult)
             tensor_tensor(nc.vector, work, "cq", last, "q", "c_t", ALU.mult)
+            add_epsilon(done)
+            scalar_then_tensor(work, "m_less_bi", gates, "d", 0.0, ALU.max, "i_sum", ALU.add)
+            reciprocal(done)
+            scalar_then_tensor(work, "h_unscaled", last, "o", 1.0, ALU.add, "cq", ALU.mult)
+            scale_rows(done)
             add_row(outs, "m_t", gates, "m_less_bi", bi_row)
             tensor_tensor(nc.gpsimd, outs, "c_t", cell, "fc", "ikv", ALU.add)
 
-            to_rows(last, "o")
             project_cols(gates, G_V, "l", "v", ACT.Identity, bias_col[:, G_V : G_V + 1], 1.0)
             leave_psum(gates, "v")
             project_cols(gates, G_O, "l", "o", ACT.Tanh, bo_half[:], 0.5)
@@ -416,12 +435,6 @@ def tile_mlstmblock_pb_t_kernel(
             leave_psum(gates, "q")
             to_rows(gates, "k")
 
-            quantise_x(ahead, "c")
-            add_epsilon(done)
-            scalar_then_tensor(work, "h_unscaled", last, "o", 1.0, ALU.add, "cq", ALU.mult)
-            reciprocal(done)
-            quantise_x(ahead, "l")
-            scale_rows(done)
             sum_of_squares(last)
             exponential(gates, "exp_minus_d", -1.0)
             exponential(gates, "exp_d", 1.0)

import math

import concourse.mybir as mybir
from concourse.masks import make_identity

FP8X4 = mybir.dt.float8_e4m3fn_x4
BF16 = mybir.dt.bfloat16
F32 = mybir.dt.float32
U32 = mybir.dt.uint32
U8 = mybir.dt.uint8
ALU = mybir.AluOpType
ACT = mybir.ActivationFunctionType

P = 128
ROWS = 4096
K = 512
H = 128
TILES = ROWS // P
TPC = 4
CHUNKS = TILES // TPC
CW = TPC * H
GATES = 6
G_I, G_F, G_K, G_Q, G_V, G_O = 0, 1, 2, 3, 4, 5
FLOPS = 2 * ROWS * K * H * GATES


def tile_mlstmblock_pb_t_kernel(
    tc,
    x_conv,
    x_left,
    c_prev,
    n_prev,
    m_prev,
    wq_w,
    wq_b,
    wk_w,
    wk_b,
    wv_w,
    wv_b,
    wi_w,
    wi_b,
    wf_w,
    wf_b,
    wo_w,
    wo_b,
    out_0,
    out_1,
    out_2,
    out_3,
):
    nc = tc.nc
    k_scale = 1.0 / math.sqrt(float(H))

    def by_partition(dram):
        return dram.rearrange("(p t) w -> p t w", t=TILES)

    x_views = {"c": by_partition(x_conv), "l": by_partition(x_left)}
    state_views = {"m": by_partition(m_prev), "n": by_partition(n_prev), "c": by_partition(c_prev)}
    out_views = {
        "h": by_partition(out_0),
        "c": by_partition(out_1),
        "n": by_partition(out_2),
        "m": by_partition(out_3),
    }
    weights = [None] * GATES
    biases = [None] * GATES
    for g, w_ap, b_ap in (
        (G_I, wi_w, wi_b),
        (G_F, wf_w, wf_b),
        (G_K, wk_w[0], wk_b),
        (G_Q, wq_w[0], wq_b),
        (G_V, wv_w[0], wv_b),
        (G_O, wo_w, wo_b),
    ):
        weights[g] = w_ap
        biases[g] = b_ap

    with tc.tile_pool(name="const", bufs=1) as const, tc.tile_pool(
        name="xin", bufs=3
    ) as xin, tc.tile_pool(name="state", bufs=CHUNKS // 2) as state, tc.tile_pool(
        name="quant", bufs=2
    ) as quant, tc.tile_pool(name="work", bufs=2) as work, tc.tile_pool(
        name="outs", bufs=3
    ) as outs, tc.psum_pool(name="front", bufs=3) as front, tc.psum_pool(
        name="gate", bufs=1
    ) as gate, tc.psum_pool(name="rows", bufs=3) as rows, tc.manual_schedule():
        kept = {}

        def absent(c):
            return c < 0 or c >= CHUNKS

        def by_tile(ap):
            return ap.rearrange("p (t h) -> p t h", h=H)

        def new(pool, name, c):
            kept[(name, c)] = pool.tile([P, CW], F32, tag=name, name=name)
            return kept[(name, c)]

        def load_x(c, nm):
            if absent(c):
                return
            x_sb = xin.tile([P, TPC * K], BF16, tag="x" + nm, name="x" + nm)
            nc.sync.dma_start(
                out=x_sb[:].rearrange("p (t k) -> p t k", t=TPC),
                in_=x_views[nm][:, c * TPC : (c + 1) * TPC, :],
            )
            kept[("x" + nm, c)] = x_sb

        def load_state(c):
            if absent(c) or c % 2 == 1:
                return
            st = state.tile([P, 2, 2, CW], BF16, tag="nc_prev", name="nc_prev")
            for s, nm in enumerate(("n", "c")):
                nc.sync.dma_start(
                    out=st[:, :, s, :],
                    in_=state_views[nm][:, c * TPC : (c + 2) * TPC, :].rearrange("p (a t) h -> p a (t h)", a=2),
                )
            kept[("nc_prev", c)] = st[:, 0, :, :]
            kept[("nc_prev", c + 1)] = st[:, 1, :, :]

        m_all = const.tile([P, CHUNKS * CW], BF16)

        def load_m(first, count):
            nc.sync.dma_start(
                out=by_tile(m_all[:, first * CW : (first + count) * CW]),
                in_=state_views["m"][:, first * TPC : (first + count) * TPC, :],
            )

        def store(c, nm):
            if absent(c):
                return
            nc.sync.dma_start(
                out=out_views[nm][:, c * TPC : (c + 1) * TPC, :], in_=by_tile(kept[(nm + "_t", c)][:])
            )

        load_x(0, "c")
        bias_rows = const.tile([P, P], BF16)
        nc.vector.memset(bias_rows[:], 0.0)
        for g in range(GATES):
            nc.sync.dma_start(out=bias_rows[g : g + 1, :], in_=biases[g].unsqueeze(0))
        w_raw = const.tile([P, GATES, 4, H], BF16)
        for g in range(GATES):
            nc.sync.dma_start(
                out=w_raw[:, g, :, :].rearrange("p (u e) c -> p u e c", u=2),
                in_=weights[g].rearrange("(u q e) c -> q u e c", u=2, e=2),
            )
        load_x(0, "l")
        load_m(0, CHUNKS // 2)
        load_state(0)
        load_x(1, "c")
        load_x(1, "l")
        load_m(CHUNKS // 2, CHUNKS // 2)
        load_x(2, "c")
        load_x(2, "l")

        zero = const.tile([P, 1], F32)
        nc.vector.memset(zero[:], 0.0)
        one = const.tile([P, 1], F32)
        nc.scalar.activation(out=one[:], in_=zero[:], func=ACT.Exp)
        half = const.tile([P, TPC], F32)
        nc.vector.memset(half[:], 0.5)
        ident = const.tile([P, P], F32)
        make_identity(nc, ident[:])
        ident_bf = const.tile([P, P], BF16)
        nc.vector.tensor_copy(out=ident_bf[:], in_=ident[:])

        bias_f32 = const.tile([P, P], F32)
        nc.vector.tensor_copy(out=bias_f32[:], in_=bias_rows[:])
        spread = rows.tile([P, CW], F32, tag="rows", name="spread")
        nc.tensor.transpose(spread[:, 0:P], bias_f32[:], ident[:])
        for g in (G_I, G_F):
            nc.tensor.matmul(
                out=spread[:, (g + 1) * P : (g + 2) * P],
                lhsT=ident_bf[:, g : g + 1].to_broadcast([P, P]),
                rhs=bias_rows[:],
                start=True,
                stop=True,
            )

        w_grouped = const.tile([P, GATES, H, 4], BF16, align_bytes=64)
        w_codes = const.tile([P, GATES * H], U32, align_bytes=64)
        w_scales = const.tile([P, GATES * H], U8, align_bytes=64)

        def quantise_weights(g0, g1):
            nc.vector.tensor_copy(
                out=w_grouped[:, g0:g1], in_=w_raw[:, g0:g1].rearrange("p g t c -> p g c t")
            )
            nc.vector.quantize_mx(
                out=w_codes[:, g0 * H : g1 * H].bitcast(FP8X4),
                scales=w_scales[:, g0 * H : g1 * H],
                in_=w_grouped[:, g0:g1].rearrange("p g c t -> p (g c t)"),
            )

        quantise_weights(G_I, G_F + 1)
        bias_col = const.tile([P, GATES], F32)
        nc.vector.tensor_copy(out=bias_col[:], in_=spread[:, 0:GATES])
        bk_scaled = const.tile([P, 1], F32)
        nc.vector.tensor_scalar_mul(out=bk_scaled[:], in0=bias_col[:, G_K : G_K + 1], scalar1=k_scale)
        bo_half = const.tile([P, 1], F32)
        nc.vector.tensor_scalar_mul(out=bo_half[:], in0=bias_col[:, G_O : G_O + 1], scalar1=0.5)
        bi_row = const.tile([P, H], F32)
        nc.vector.tensor_copy(out=bi_row[:], in_=spread[:, (G_I + 1) * P : (G_I + 2) * P])
        bf_minus_bi_row = const.tile([P, H], F32)
        nc.vector.tensor_tensor(
            out=bf_minus_bi_row[:], in0=spread[:, (G_F + 1) * P : (G_F + 2) * P], in1=bi_row[:], op=ALU.subtract
        )
        quantise_weights(G_K, G_Q + 1)
        quantise_weights(G_V, G_O + 1)

        def over_tiles(row):
            return row[:].unsqueeze(1).to_broadcast([P, TPC, H])

        m_shifted = const.tile([P, CHUNKS * CW], F32)
        for c in range(CHUNKS):
            nc.gpsimd.tensor_tensor(
                out=by_tile(m_shifted[:, c * CW : (c + 1) * CW]),
                in0=by_tile(m_all[:, c * CW : (c + 1) * CW]),
                in1=over_tiles(bf_minus_bi_row),
                op=ALU.add,
            )
            kept[("m_shifted", c)] = m_shifted[:, c * CW : (c + 1) * CW]

        def transpose_x(c, nm, half_no):
            if absent(c):
                return
            words = kept[("x" + nm, c)][:].bitcast(F32)
            bank = front.tile([P, CW], F32, tag="front", name="xT")
            for tt in range(2):
                t = 2 * half_no + tt
                for u in range(2):
                    nc.tensor.transpose(
                        bank[:, u * 256 + tt * P : u * 256 + (tt + 1) * P],
                        words[:, t * 256 + u * P : t * 256 + (u + 1) * P],
                        ident[:],
                    )
            kept[("xT" + nm, c, half_no)] = bank

        def regroup_x(c, nm, half_no):
            if absent(c):
                return
            if ("grouped", c) not in kept:
                kept[("grouped", c)] = quant.tile([P, 2 * 4 * CW], BF16, tag="grouped", name="grouped", align_bytes=64)
            words = kept[("grouped", c)][:].bitcast(F32)
            part = 2 * ("c", "l").index(nm) + half_no
            nc.scalar.copy(
                out=words[:, part * CW : (part + 1) * CW].rearrange("p (b u) -> p b u", u=2),
                in_=kept[("xT" + nm, c, half_no)][:].rearrange("p (u b) -> p b u", u=2),
            )

        def quantise_x(c):
            if absent(c):
                return
            codes = quant.tile([P, 2 * CW], U32, tag="codes", name="codes", align_bytes=64)
            scales = quant.tile([P, 2 * CW], U8, tag="scales", name="scales", align_bytes=64)
            nc.vector.quantize_mx(out=codes[:].bitcast(FP8X4), scales=scales[:], in_=kept[("grouped", c)][:])
            kept[("mxc", c)] = (codes[:, 0:CW], scales[:, 0:CW])
            kept[("mxl", c)] = (codes[:, CW : 2 * CW], scales[:, CW : 2 * CW])

        def project_rows(c, g, nm, name):
            if absent(c):
                return
            codes, scales = kept[("mx" + nm, c)]
            acc = gate.tile([P, CW], F32, tag=name, name=name)
            for t in range(TPC):
                nc.tensor.matmul_mx(
                    out=acc[:, t * H : (t + 1) * H],
                    lhsT=codes[:, t * P : (t + 1) * P].bitcast(FP8X4),
                    lhsT_scale=scales[:, t * P : (t + 1) * P],
                    rhs=w_codes[:, g * H : (g + 1) * H].bitcast(FP8X4),
                    rhs_scale=w_scales[:, g * H : (g + 1) * H],
                    start=True,
                    stop=True,
                )
            kept[(name, c)] = acc

        def project_cols(c, g, nm, name, func, bias_ap, scale):
            if absent(c):
                return
            codes, scales = kept[("mx" + nm, c)]
            acc = front.tile([P, CW], F32, tag="front", name="acc")
            nc.tensor.matmul_mx(
                out=acc[:],
                lhsT=w_codes[:, g * H : (g + 1) * H].bitcast(FP8X4),
                lhsT_scale=w_scales[:, g * H : (g + 1) * H],
                rhs=codes[:].bitcast(FP8X4),
                rhs_scale=scales[:],
                start=True,
                stop=True,
            )
            kept[("acc" + name, c)] = (acc, func, bias_ap, scale)

        def leave_psum(c, name):
            if absent(c):
                return
            acc, func, bias_ap, scale = kept[("acc" + name, c)]
            nc.scalar.activation(
                out=new(work, name + "_cols", c)[:], in_=acc[:], func=func, bias=bias_ap, scale=scale
            )

        def to_rows(c, name):
            if absent(c):
                return
            src = kept[(name + "_cols", c)]
            bank = rows.tile([P, CW], F32, tag="rows", name=name + "_rows")
            for t in range(TPC):
                nc.tensor.transpose(bank[:, t * H : (t + 1) * H], src[:, t * P : (t + 1) * P], ident[:])
            kept[(name, c)] = bank

        def tensor_tensor(engine, pool, out_name, c, a, b, op):
            if absent(c):
                return
            engine.tensor_tensor(out=new(pool, out_name, c)[:], in0=kept[(a, c)][:], in1=kept[(b, c)][:], op=op)

        def scalar_then_tensor(pool, out_name, c, a, scalar, op0, b, op1):
            if absent(c):
                return
            nc.vector.scalar_tensor_tensor(
                out=new(pool, out_name, c)[:],
                in0=kept[(a, c)][:],
                scalar=scalar,
                in1=kept[(b, c)][:],
                op0=op0,
                op1=op1,
            )

        def add_row(pool, out_name, c, a, row):
            if absent(c):
                return
            nc.gpsimd.tensor_tensor(
                out=by_tile(new(pool, out_name, c)[:]), in0=by_tile(kept[(a, c)][:]), in1=over_tiles(row), op=ALU.add
            )

        def forget_states(c):
            if absent(c):
                return
            both = work.tile([P, 2 * CW], F32, tag="f_states", name="f_states")
            nc.vector.scalar_tensor_tensor(
                out=both[:].rearrange("p (s w) -> p s w", s=2),
                in0=kept[("exp_d", c)][:].unsqueeze(1).to_broadcast([P, 2, CW]),
                scalar=1.0,
                in1=kept[("nc_prev", c)],
                op0=ALU.min,
                op1=ALU.mult,
            )
            kept[("fn", c)] = both[:, 0:CW]
            kept[("fc", c)] = both[:, CW : 2 * CW]

        def exponential(c, out_name, sign):
            if absent(c):
                return
            nc.scalar.activation(out=new(work, out_name, c)[:], in_=kept[("d", c)][:], func=ACT.Exp, scale=sign)

        def sum_of_squares(c):
            if absent(c):
                return
            squares = work.tile([P, CW], F32, tag="squares", name="squares")
            ss = work.tile([P, TPC], F32, tag="ss", name="ss")
            for t in range(TPC):
                nc.scalar.activation(
                    out=squares[:, t * H : (t + 1) * H],
                    in_=kept[("nq", c)][:, t * H : (t + 1) * H],
                    func=ACT.Square,
                    scale=2.0,
                    accum_out=ss[:, t : t + 1],
                )
            kept[("ss", c)] = ss

        def small(c, name):
            kept[(name, c)] = work.tile([P, TPC], F32, tag=name, name=name)
            return kept[(name, c)]

        def square_root(c):
            if absent(c):
                return
            nc.gpsimd.tensor_tensor(out=small(c, "root")[:], in0=kept[("ss", c)][:], in1=half[:], op=ALU.pow)

        def add_epsilon(c):
            if absent(c):
                return
            nc.vector.tensor_scalar_add(out=small(c, "denom2")[:], in0=kept[("root", c)][:], scalar1=2.0e-6)

        def reciprocal(c):
            if absent(c):
                return
            nc.vector.reciprocal(out=small(c, "scale")[:], in_=kept[("denom2", c)][:])

        def scale_rows(c):
            if absent(c):
                return
            nc.vector.tensor_tensor(
                out=by_tile(new(outs, "h_t", c)[:]),
                in0=by_tile(kept[("h_unscaled", c)][:]),
                in1=kept[("scale", c)][:].unsqueeze(2).to_broadcast([P, TPC, H]),
                op=ALU.mult,
            )

        for j in range(-3, CHUNKS + 2):
            far, ahead, gates, cell, last, done = j + 3, j + 2, j + 1, j, j - 1, j - 2

            quantise_x(ahead)
            tensor_tensor(nc.vector, work, "u", gates, "f_sum", "m_shifted", ALU.add)
            scalar_then_tensor(work, "ik", cell, "exp_minus_d", 1.0, ALU.min, "k", ALU.mult)
            tensor_tensor(nc.vector, work, "d", gates, "u", "i_sum", ALU.subtract)
            forget_states(cell)
            tensor_tensor(nc.vector, work, "nq", last, "q", "n_t", ALU.mult)
            leave_psum(gates, "k")
            to_rows(cell, "v")
            tensor_tensor(nc.gpsimd, outs, "n_t", cell, "fn", "ik", ALU.add)

            for nm in ("c", "l"):
                for half_no in range(2):
                    transpose_x(far, nm, half_no)
                    regroup_x(far, nm, half_no)
            to_rows(last, "o")
            load_x(j + 6, "c")
            load_x(j + 6, "l")
            load_state(j + 4)
            store(cell, "n")

            tensor_tensor(nc.vector, work, "ikv", cell, "v", "ik", ALU.mult)
            tensor_tensor(nc.vector, work, "cq", last, "q", "c_t", ALU.mult)
            add_epsilon(done)
            scalar_then_tensor(work, "m_less_bi", gates, "d", 0.0, ALU.max, "i_sum", ALU.add)
            reciprocal(done)
            scalar_then_tensor(work, "h_unscaled", last, "o", 1.0, ALU.add, "cq", ALU.mult)
            scale_rows(done)
            add_row(outs, "m_t", gates, "m_less_bi", bi_row)
            tensor_tensor(nc.gpsimd, outs, "c_t", cell, "fc", "ikv", ALU.add)

            project_cols(gates, G_V, "l", "v", ACT.Identity, bias_col[:, G_V : G_V + 1], 1.0)
            leave_psum(gates, "v")
            project_cols(gates, G_O, "l", "o", ACT.Tanh, bo_half[:], 0.5)
            leave_psum(gates, "o")
            project_cols(gates, G_Q, "c", "q", ACT.Identity, bias_col[:, G_Q : G_Q + 1], 1.0)
            leave_psum(gates, "q")
            to_rows(gates, "k")

            sum_of_squares(last)
            exponential(gates, "exp_minus_d", -1.0)
            exponential(gates, "exp_d", 1.0)
            square_root(last)
            store(gates, "m")
            store(cell, "c")
            store(done, "h")

            project_rows(ahead, G_F, "c", "f_sum")
            project_rows(ahead, G_I, "c", "i_sum")
            project_cols(ahead, G_K, "c", "k", ACT.Identity, bk_scaled[:], k_scale)
            to_rows(cell, "q")
